import numpy as np
import ml_dtypes


def mxq(x, axis, fmt="e4m3"):
    dtype, down = {"e4m3": (ml_dtypes.float8_e4m3fn, 7), "e5m2": (ml_dtypes.float8_e5m2, 14)}[fmt]
    v = np.moveaxis(np.asarray(x, np.float32).astype(ml_dtypes.bfloat16).astype(np.float64), axis, -1)
    blocks = v.reshape(v.shape[:-1] + (-1, 32))
    amax = np.abs(blocks).max(-1, keepdims=True)
    byte = np.maximum(np.where(amax > 0, np.frexp(amax)[1] - 1 + 127, 0) - down, 1)
    scale = np.exp2(byte - 127.0)
    codes = (blocks / scale).astype(np.float32).astype(dtype).astype(np.float64)
    return np.moveaxis((codes * scale).reshape(v.shape), -1, axis)


WIDE = False


def mx_kscale(k):
    if not WIDE:
        return np.ones(k)
    levels = np.array([10, -10, 5, -5, 0])
    if k % 512:
        return np.exp2(np.random.permutation(np.resize(levels, k // 32))).repeat(32)
    a = np.empty((k // 512, 16))
    for p in range(k // 512):
        a[p, :8] = np.random.permutation(np.resize(levels, 8))
        for g in range(8):
            far = levels[np.abs(levels - a[p, g]) >= 10]
            a[p, g + 8] = far[np.random.randint(len(far))]
    return np.exp2(a.ravel()).repeat(32)


BF16 = ml_dtypes.bfloat16


def bf(x):
    return np.asarray(x, np.float32).astype(BF16)


def f64(x):
    return np.asarray(x).astype(np.float64)


B, L, D, O = 16, 256, 512, 2


def setup_inputs():
    s = mx_kscale(D)
    u = mx_kscale(D)
    w = np.random.standard_normal((O, D + 1, D))
    w[:, :D, :] *= 3.0 / D / s[:, None]
    w[:, D, :] *= 1.0 / np.sqrt(D)
    return {"x1": bf(np.random.standard_normal((B, L, D)) * s),
            "x2": bf(np.random.standard_normal((B, L, D)) / u),
            "bw": bf(np.random.uniform(size=(2,))),
            "W_bil": bf(w * u),
            "t_ones": bf(np.random.standard_normal((B, L, O))),
            "lin1": bf(np.random.standard_normal((B, L, O))),
            "lin2": bf(np.random.standard_normal((B, L, O))),
            "b_lin": bf(np.random.standard_normal(O) * 0.5)}


def reference(x1, x2, bw, W_bil, t_ones, lin1, lin2, b_lin):
    e = np.exp(f64(bw) - f64(bw).max())
    bwn = e / e.sum()
    w = f64(W_bil)
    t = (mxq(f64(x1).reshape(B * L, D), 1, "e4m3") @ mxq(w[:, :D, :], 1, "e4m3")) + w[:, D, :][:, None, :]
    t = t.reshape(O, B, L, D)
    pair = mxq(t, 3, "e4m3") @ mxq(f64(x2), 2, "e4m3").transpose(0, 2, 1)
    bil = pair.transpose(1, 2, 3, 0) + f64(t_ones)[:, :, None, :]
    lin = f64(lin1)[:, :, None, :] + f64(lin2)[:, None, :, :] + f64(b_lin)
    return bwn[0] * bil + bwn[1] * lin

@@ -1,0 +1,422 @@
+from contextlib import ExitStack
+
+import concourse.mybir as mybir
+from concourse.masks import make_identity
+
+F32 = mybir.dt.float32
+BF16 = mybir.dt.bfloat16
+U32 = mybir.dt.uint32
+U8 = mybir.dt.uint8
+FP8X4 = mybir.dt.float8_e4m3fn_x4
+ACT = mybir.ActivationFunctionType
+ALU = mybir.AluOpType
+
+P = 128
+B, L, D, O = 16, 256, 512, 2
+H = L // P
+
+FLOPS = 2 * B * L * D * O * D + 2 * B * O * L * L * D
+
+LOAD_GROUPS = [(1, 1), (2, 1), (3, 1), (4, 2), (6, 2), (8, 2), (10, 2), (12, 2), (14, 2)]
+REGROUP_ENGINE = "gpsimd"
+
+
+def tile_biaffine_pa_t_kernel(tc, x1, x2, bw, W_bil, t_ones, lin1, lin2, b_lin, out):
+    nc = tc.nc
+    with ExitStack() as ctx:
+        const = ctx.enter_context(tc.tile_pool(name="const", bufs=1))
+        stage = ctx.enter_context(tc.tile_pool(name="stage", bufs=2))
+        keep3 = ctx.enter_context(tc.tile_pool(name="keep3", bufs=3))
+        keep4 = ctx.enter_context(tc.tile_pool(name="keep4", bufs=4))
+        ps_t = ctx.enter_context(tc.psum_pool(name="ps_t", bufs=4))
+        ps_1 = ctx.enter_context(tc.psum_pool(name="ps_1", bufs=2))
+        ps_2 = ctx.enter_context(tc.psum_pool(name="ps_2", bufs=2))
+
+        sm = const.tile([P, 256], F32, name="sm")
+        nc.vector.memset(sm[:], 0.0)
+        ident = const.tile([P, P], F32, name="ident")
+        make_identity(nc, ident[:])
+        ident_bf = const.tile([P, P], BF16, name="ident_bf")
+        make_identity(nc, ident_bf[:])
+        l2r = const.tile([P, L * O], BF16, name="l2r")
+        nc.vector.memset(l2r[:], 0.0)
+
+        w_raw = []
+        for o in range(O):
+            wr = const.tile([P, 4, D], BF16, name="w_raw%d" % o)
+            w_raw.append(wr)
+        x1_raw = {}
+        x2_raw = {}
+
+        def load_w(o):
+            nc.sync.dma_start(
+                out=w_raw[o][:].rearrange("q t j -> q (t j)"),
+                in_=W_bil[o, 0:D, :].rearrange("(q t) j -> q (t j)", t=4),
+            )
+
+        def load_x(src, store, label, b0, nb):
+            xr = const.tile([P, nb, H * D], BF16, name="%s_raw%d" % (label, b0))
+            nc.sync.dma_start(out=xr[:], in_=src[b0 : b0 + nb].rearrange("b (p h) i -> p b (h i)", h=H))
+            for k in range(nb):
+                store[b0 + k] = (xr, k)
+
+        sm_bf = sm[:].bitcast(BF16)
+        bw_b = const.tile([P, 2], BF16, name="bw_b")
+        bl_b = const.tile([P, 2], BF16, name="bl_b")
+        nc.scalar.dma_start(out=bw_b[:], in_=bw.partition_broadcast(P))
+        nc.scalar.dma_start(out=sm_bf[64:66, :], in_=W_bil[:, D, :])
+        nc.scalar.dma_start(out=sm_bf[0:16, :], in_=t_ones.rearrange("b x o -> b (x o)"))
+        nc.scalar.dma_start(out=sm_bf[32:48, :], in_=lin1.rearrange("b x o -> b (x o)"))
+
+        load_w(0)
+        load_x(x1, x1_raw, "x1", 0, 1)
+        load_w(1)
+        load_x(x2, x2_raw, "x2", 0, 1)
+        nc.scalar.dma_start(out=bl_b[:], in_=b_lin.partition_broadcast(P))
+        nc.scalar.dma_start(out=l2r[0:B, :], in_=lin2.rearrange("b y o -> b (y o)"))
+        for b0, nb in LOAD_GROUPS:
+            load_x(x1, x1_raw, "x1", b0, nb)
+            load_x(x2, x2_raw, "x2", b0, nb)
+
+        bwf = const.tile([P, 2], F32, name="bwf")
+        nc.vector.tensor_copy(out=bwf[:], in_=bw_b[:])
+        negm = const.tile([P, 1], F32, name="negm")
+        nc.vector.tensor_tensor(out=negm[:], in0=bwf[:, 0:1], in1=bwf[:, 1:2], op=ALU.max)
+        nc.vector.tensor_scalar_mul(out=negm[:], in0=negm[:], scalar1=-1.0)
+        ebw = const.tile([P, 2], F32, name="ebw")
+        nc.scalar.activation(out=ebw[:], in_=bwf[:], func=ACT.Exp, bias=negm[:], scale=1.0)
+
+        sm_t = ps_t.tile([P, 4, P], F32, name="pt", tag="pt")
+        sm_h = sm[:].rearrange("p (r h) -> p h r", h=H)
+        for h in range(H):
+            nc.tensor.transpose(out=sm_t[:, h, :], in_=sm_h[:, h, :], identity=ident[:])
+        for u in range(2):
+            nc.tensor.transpose(out=sm_t[:, 2 + u, :], in_=sm[:, u : 2 * P : 2], identity=ident[:])
+        sm_s = const.tile([P, 4, P], F32, name="sm_s")
+        nc.vector.tensor_copy(out=sm_s[:], in_=sm_t[:])
+        sm_v = sm_s[:].bitcast(BF16).rearrange("p k (row e) -> p k row e", e=2)
+        bias_f = const.tile([P, O, 4], F32, name="bias_f")
+        bias_v = bias_f[:].rearrange("p o (u e) -> p u o e", u=2)
+        for u in range(2):
+            nc.vector.tensor_copy(out=bias_v[:, u], in_=sm_v[:, 2 + u, 64:66, :])
+
+        w_q = const.tile([P, O * D], U32, name="w_q", align_bytes=64)
+        w_s = const.tile([P, O * D], U8, name="w_s", align_bytes=64)
+        w_g = []
+        for o in range(O):
+            wg = const.tile([P, 4 * D], BF16, name="w_g%d" % o, align_bytes=64)
+            w_g.append(wg)
+
+        def regroup_w(o, uj, engine):
+            dst = w_g[o][:].rearrange("q (uj ej m t) -> q uj ej m t", uj=2, ej=2, t=4)
+            src = w_raw[o][:].rearrange("q t (m uj ej) -> q uj ej m t", uj=2, ej=2)
+            if engine == "vector":
+                nc.vector.tensor_copy(out=dst[:, uj], in_=src[:, uj])
+            elif engine == "scalar":
+                nc.scalar.copy(out=dst[:, uj], in_=src[:, uj])
+            else:
+                nc.gpsimd.tensor_scalar(
+                    out=dst[:, uj], in0=src[:, uj], scalar1=1.0, scalar2=0.0, op0=ALU.mult, op1=ALU.add
+                )
+
+        def quant_w(o):
+            nc.vector.quantize_mx(
+                out=w_q[:, o * D : (o + 1) * D].bitcast(FP8X4),
+                scales=w_s[:, o * D : (o + 1) * D],
+                in_=w_g[o][:],
+            )
+
+        pt_x = {}
+        xg = {}
+        xq = {}
+        p1 = {}
+        tg = {}
+        tq = {}
+        p2 = {}
+        pp = {}
+        tp = {}
+        st = {}
+
+        def transposes(b):
+            for which, store in ((0, x1_raw), (1, x2_raw)):
+                xr, k = store[b]
+                words = xr[:].bitcast(F32)
+                pt = ps_t.tile([P, H, 2, P], F32, name="pt", tag="pt")
+                for h in range(H):
+                    for u in range(2):
+                        c0 = h * 256
+                        nc.tensor.transpose(
+                            out=pt[:, h, u, :], in_=words[:, k, c0 + u : c0 + 256 : 2], identity=ident[:]
+                        )
+                pt_x[(b, which)] = pt
+
+        def exit_x1(b):
+            x1g = stage.tile([P, 4 * L], BF16, name="x1g", align_bytes=64)
+            nc.scalar.copy(
+                out=x1g[:].bitcast(F32).rearrange("q (h r u) -> q h r u", h=H, u=2),
+                in_=pt_x[(b, 0)][:].rearrange("q h u r -> q h r u"),
+            )
+            xg[(b, 0)] = x1g
+
+        def exit_x2(b):
+            x2g = stage.tile([P, 4 * L], BF16, name="x2g", align_bytes=64)
+            nc.scalar.copy(
+                out=x2g[:].bitcast(F32).rearrange("q (r h u) -> q r h u", h=H, u=2),
+                in_=pt_x[(b, 1)][:].rearrange("q h u r -> q r h u"),
+            )
+            xg[(b, 1)] = x2g
+
+        def quant_x1(b):
+            x1q = keep3.tile([P, L], U32, name="x1q", align_bytes=64)
+            x1s = keep3.tile([P, L], U8, name="x1s", align_bytes=64)
+            nc.vector.quantize_mx(out=x1q[:].bitcast(FP8X4), scales=x1s[:], in_=xg[(b, 0)][:])
+            xq[(b, 0)] = (x1q, x1s)
+
+        def quant_x2(b):
+            x2q = keep4.tile([P, L], U32, name="x2q", align_bytes=64)
+            x2s = keep4.tile([P, L], U8, name="x2s", align_bytes=64)
+            nc.vector.quantize_mx(out=x2q[:].bitcast(FP8X4), scales=x2s[:], in_=xg[(b, 1)][:])
+            xq[(b, 1)] = (x2q, x2s)
+
+        def stage1(b, g):
+            o, h = g // H, g % H
+            x1q, x1s = xq[(b, 0)]
+            acc = ps_1.tile([P, 4, P], F32, name="p1", tag="p1")
+            for c in range(4):
+                w0 = (o * 4 + c) * P
+                nc.tensor.matmul_mx(
+                    out=acc[:, c, :],
+                    lhsT=w_q[:, w0 : w0 + P].bitcast(FP8X4),
+                    lhsT_scale=w_s[:, w0 : w0 + P],
+                    rhs=x1q[:, h * P : (h + 1) * P].bitcast(FP8X4),
+                    rhs_scale=x1s[:, h * P : (h + 1) * P],
+                    start=True,
+                    stop=True,
+                )
+            p1[(b, g)] = acc
+
+        def get_tg(b):
+            if b not in tg:
+                tgt = stage.tile([P, 4 * O * L], BF16, name="tg", align_bytes=64)
+                tg[b] = tgt
+            return tg[b]
+
+        def t_out(b, g):
+            o = g // H
+            view = get_tg(b)[:].rearrange("q (g r c) -> q g r c", g=O * H, c=4)
+            nc.vector.tensor_tensor(
+                out=view[:, g],
+                in0=p1[(b, g)][:].rearrange("q c r -> q r c"),
+                in1=bias_f[:, o, :].unsqueeze(1).to_broadcast([P, P, 4]),
+                op=ALU.add,
+            )
+
+        def quant_t(b):
+            tqt = stage.tile([P, O * L], U32, name="tq", align_bytes=64)
+            tst = stage.tile([P, O * L], U8, name="ts", align_bytes=64)
+            nc.vector.quantize_mx(out=tqt[:].bitcast(FP8X4), scales=tst[:], in_=tg[b][:])
+            tq[b] = (tqt, tst)
+
+        def stage2(b):
+            tqt, tst = tq[b]
+            x2q, x2s = xq[(b, 1)]
+            for h in range(H):
+                acc = ps_2.tile([P, O, L], F32, name="p2", tag="p2")
+                for o in range(O):
+                    c0 = (o * H + h) * P
+                    nc.tensor.matmul_mx(
+                        out=acc[:, o, :],
+                        lhsT=tqt[:, c0 : c0 + P].bitcast(FP8X4),
+                        lhsT_scale=tst[:, c0 : c0 + P],
+                        rhs=x2q[:].bitcast(FP8X4),
+                        rhs_scale=x2s[:],
+                        start=True,
+                        stop=True,
+                    )
+                p2[(b, h)] = acc
+
+        def planar_pe(b):
+            x1q, x1s = xq[(b, 0)]
+            for cp in range(2):
+                acc = ps_t.tile([P, 2, L], F32, name="pt", tag="pt")
+                for ci in range(2):
+                    w0 = (4 + 2 * cp + ci) * P
+                    nc.tensor.matmul_mx(
+                        out=acc[:, ci, :],
+                        lhsT=w_q[:, w0 : w0 + P].bitcast(FP8X4),
+                        lhsT_scale=w_s[:, w0 : w0 + P],
+                        rhs=x1q[:].bitcast(FP8X4),
+                        rhs_scale=x1s[:],
+                        start=True,
+                        stop=True,
+                    )
+                pp[(b, cp)] = acc
+
+        def planar_exits(b):
+            tpt = stage.tile([P, 4, L], BF16, name="tp")
+            for c in range(4):
+                nc.scalar.activation(
+                    out=tpt[:, c, :],
+                    in_=pp[(b, c // 2)][:, c % 2, :],
+                    func=ACT.Identity,
+                    bias=bias_f[:, 1, c : c + 1],
+                    scale=1.0,
+                )
+            tp[b] = tpt
+
+        def regroup_t(b):
+            dst = get_tg(b)[:, 4 * L : 8 * L].rearrange("q (xb i t) -> q xb t i", i=4, t=4)
+            src = tp[b][:].rearrange("q t (xb i) -> q xb t i", i=4)
+            if REGROUP_ENGINE == "vector":
+                nc.vector.tensor_copy(out=dst, in_=src)
+            else:
+                dst = get_tg(b)[:, 4 * L : 8 * L].rearrange("q (x t) -> q x t", t=4)
+                src = tp[b][:].rearrange("q t x -> q x t")
+                for k in range(2):
+                    nc.gpsimd.tensor_scalar(
+                        out=dst[:, P * k : P * k + P],
+                        in0=src[:, P * k : P * k + P],
+                        scalar1=1.0,
+                        scalar2=0.0,
+                        op0=ALU.mult,
+                        op1=ALU.add,
+                    )
+
+        def spread_lin2(b):
+            acc = ps_t.tile([P, L, O], F32, name="pt", tag="pt")
+            nc.tensor.matmul(
+                out=acc[:].rearrange("p y o -> p (y o)"),
+                lhsT=ident_bf[:, b : b + 1].to_broadcast([P, P]),
+                rhs=l2r[:],
+                start=True,
+                stop=True,
+            )
+            stt = keep3.tile([P, H, O, L], F32, name="st")
+            for h in range(H):
+                for o in range(O):
+                    nc.scalar.activation(
+                        out=stt[:, h, o, :],
+                        in_=acc[:, :, o],
+                        func=ACT.Identity,
+                        bias=a_x[:, h, b, o : o + 1],
+                        scale=bwn[:, 1:2],
+                    )
+            st[b] = stt
+
+        def out_exit(b):
+            ot = keep4.tile([P, H, L, O], F32, name="ot")
+            for h in range(H):
+                nc.vector.scalar_tensor_tensor(
+                    out=ot[:, h],
+                    in0=p2[(b, h)][:].rearrange("p o y -> p y o"),
+                    scalar=bwn[:, 0:1],
+                    in1=st[b][:, h].rearrange("p o y -> p y o"),
+                    op0=ALU.mult,
+                    op1=ALU.add,
+                )
+                if b == B - 1:
+                    nc.sync.dma_start(
+                        out=out[b].rearrange("(p h) y o -> p h (y o)", h=H)[:, h, :],
+                        in_=ot[:, h].rearrange("p y o -> p (y o)"),
+                    )
+            if b < B - 1:
+                nc.sync.dma_start(
+                    out=out[b].rearrange("(p h) y o -> p (h y o)", h=H),
+                    in_=ot[:].rearrange("p h y o -> p (h y o)"),
+                )
+
+        def softmax_tail():
+            nc.vector.tensor_tensor(out=esum[:], in0=ebw[:, 0:1], in1=ebw[:, 1:2], op=ALU.add)
+            nc.vector.reciprocal(out=rsum[:], in_=esum[:])
+            nc.vector.tensor_scalar_mul(out=bwn[:], in0=ebw[:], scalar1=rsum[:])
+            nc.vector.tensor_copy(out=blf[:], in_=bl_b[:])
+            for h in range(H):
+                nc.vector.tensor_tensor(
+                    out=a_x[:, h],
+                    in0=sm_v[:, h, 32:48, :],
+                    in1=blf[:].unsqueeze(1).to_broadcast([P, B, O]),
+                    op=ALU.add,
+                )
+            a_flat = a_x[:].rearrange("p h b o -> p (h b o)")
+            nc.vector.tensor_scalar_mul(out=a_flat, in0=a_flat, scalar1=bwn[:, 1:2])
+            for h in range(H):
+                nc.vector.scalar_tensor_tensor(
+                    out=a_x[:, h],
+                    in0=sm_v[:, h, 0:16, :],
+                    scalar=bwn[:, 0:1],
+                    in1=a_x[:, h],
+                    op0=ALU.mult,
+                    op1=ALU.add,
+                )
+
+        esum = const.tile([P, 1], F32, name="esum")
+        rsum = const.tile([P, 1], F32, name="rsum")
+        bwn = const.tile([P, 2], F32, name="bwn")
+        blf = const.tile([P, 2], F32, name="blf")
+        a_x = const.tile([P, H, B, O], F32, name="a_x")
+
+        regroup_w(0, 0, "vector")
+        regroup_w(0, 1, "vector")
+        transposes(0)
+        exit_x1(0)
+        regroup_w(1, 0, "scalar")
+        regroup_w(1, 1, "gpsimd")
+        exit_x2(0)
+        quant_w(0)
+        quant_x1(0)
+        stage1(0, 0)
+        stage1(0, 1)
+        transposes(1)
+        exit_x1(1)
+        exit_x2(1)
+
+        t_out(0, 0)
+        t_out(0, 1)
+        quant_w(1)
+        quant_x2(0)
+        quant_x1(1)
+        quant_x2(1)
+        softmax_tail()
+        planar_pe(0)
+        planar_exits(0)
+        regroup_t(0)
+        transposes(2)
+        exit_x1(2)
+        exit_x2(2)
+        planar_pe(1)
+        stage1(1, 0)
+        stage1(1, 1)
+        planar_exits(1)
+        regroup_t(1)
+        spread_lin2(0)
+        spread_lin2(1)
+        quant_x1(2)
+        quant_x2(2)
+        quant_t(0)
+        transposes(3)
+
+        for b in range(1, B + 1):
+            stage2(b - 1)
+            if b + 2 < B:
+                exit_x1(b + 2)
+                exit_x2(b + 2)
+            if b + 1 < B:
+                planar_pe(b + 1)
+            if b < B:
+                for g in range(H):
+                    t_out(b, g)
+                    if b + 1 < B:
+                        stage1(b + 1, g)
+            if b + 1 < B:
+                planar_exits(b + 1)
+                regroup_t(b + 1)
+            out_exit(b - 1)
+            if b + 1 < B:
+                spread_lin2(b + 1)
+            if b + 2 < B:
+                quant_x1(b + 2)
+                quant_x2(b + 2)
+            if b < B:
+                quant_t(b)
+            if b + 3 < B:
+                transposes(b + 3)

@@ -18,7 +18,6 @@ H = L // P
 FLOPS = 2 * B * L * D * O * D + 2 * B * O * L * L * D
 
 LOAD_GROUPS = [(1, 1), (2, 1), (3, 1), (4, 2), (6, 2), (8, 2), (10, 2), (12, 2), (14, 2)]
-REGROUP_ENGINE = "gpsimd"
 
 
 def tile_biaffine_pa_t_kernel(tc, x1, x2, bw, W_bil, t_ones, lin1, lin2, b_lin, out):
@@ -31,15 +30,19 @@ def tile_biaffine_pa_t_kernel(tc, x1, x2, bw, W_bil, t_ones, lin1, lin2, b_lin, 
         ps_t = ctx.enter_context(tc.psum_pool(name="ps_t", bufs=4))
         ps_1 = ctx.enter_context(tc.psum_pool(name="ps_1", bufs=2))
         ps_2 = ctx.enter_context(tc.psum_pool(name="ps_2", bufs=2))
+        ctx.enter_context(tc.manual_schedule())
 
+        warm = const.tile([P, 1], F32, name="warm")
+        nc.vector.memset(warm[:], 0.0)
+        warm_o = const.tile([P, 1], F32, name="warm_o")
         sm = const.tile([P, 256], F32, name="sm")
         nc.vector.memset(sm[:], 0.0)
+        l2r = const.tile([P, L * O], BF16, name="l2r")
+        nc.vector.memset(l2r[:], 0.0)
         ident = const.tile([P, P], F32, name="ident")
         make_identity(nc, ident[:])
         ident_bf = const.tile([P, P], BF16, name="ident_bf")
         make_identity(nc, ident_bf[:])
-        l2r = const.tile([P, L * O], BF16, name="l2r")
-        nc.vector.memset(l2r[:], 0.0)
 
         w_raw = []
         for o in range(O):
@@ -63,42 +66,25 @@ def tile_biaffine_pa_t_kernel(tc, x1, x2, bw, W_bil, t_ones, lin1, lin2, b_lin, 
         sm_bf = sm[:].bitcast(BF16)
         bw_b = const.tile([P, 2], BF16, name="bw_b")
         bl_b = const.tile([P, 2], BF16, name="bl_b")
-        nc.scalar.dma_start(out=bw_b[:], in_=bw.partition_broadcast(P))
-        nc.scalar.dma_start(out=sm_bf[64:66, :], in_=W_bil[:, D, :])
-        nc.scalar.dma_start(out=sm_bf[0:16, :], in_=t_ones.rearrange("b x o -> b (x o)"))
-        nc.scalar.dma_start(out=sm_bf[32:48, :], in_=lin1.rearrange("b x o -> b (x o)"))
+        bias_b = const.tile([P, O, 4], BF16, name="bias_b")
 
-        load_w(0)
         load_x(x1, x1_raw, "x1", 0, 1)
+        load_w(0)
         load_w(1)
+        nc.sync.dma_start(out=bias_b[:], in_=W_bil[:, D, :].rearrange("o (p c) -> p o c", c=4))
+        nc.sync.dma_start(out=bw_b[:], in_=bw.partition_broadcast(P))
+        nc.sync.dma_start(out=sm_bf[0:16, :], in_=t_ones.rearrange("b x o -> b (x o)"))
+        nc.sync.dma_start(out=sm_bf[32:48, :], in_=lin1.rearrange("b x o -> b (x o)"))
         load_x(x2, x2_raw, "x2", 0, 1)
-        nc.scalar.dma_start(out=bl_b[:], in_=b_lin.partition_broadcast(P))
-        nc.scalar.dma_start(out=l2r[0:B, :], in_=lin2.rearrange("b y o -> b (y o)"))
-        for b0, nb in LOAD_GROUPS:
+        nc.sync.dma_start(out=bl_b[:], in_=b_lin.partition_broadcast(P))
+        nc.sync.dma_start(out=l2r[0:B, :], in_=lin2.rearrange("b y o -> b (y o)"))
+        load_x(x1, x1_raw, "x1", 1, 1)
+        load_x(x2, x2_raw, "x2", 1, 1)
+        for b0, nb in LOAD_GROUPS[1:]:
             load_x(x1, x1_raw, "x1", b0, nb)
             load_x(x2, x2_raw, "x2", b0, nb)
 
-        bwf = const.tile([P, 2], F32, name="bwf")
-        nc.vector.tensor_copy(out=bwf[:], in_=bw_b[:])
-        negm = const.tile([P, 1], F32, name="negm")
-        nc.vector.tensor_tensor(out=negm[:], in0=bwf[:, 0:1], in1=bwf[:, 1:2], op=ALU.max)
-        nc.vector.tensor_scalar_mul(out=negm[:], in0=negm[:], scalar1=-1.0)
-        ebw = const.tile([P, 2], F32, name="ebw")
-        nc.scalar.activation(out=ebw[:], in_=bwf[:], func=ACT.Exp, bias=negm[:], scale=1.0)
-
-        sm_t = ps_t.tile([P, 4, P], F32, name="pt", tag="pt")
-        sm_h = sm[:].rearrange("p (r h) -> p h r", h=H)
-        for h in range(H):
-            nc.tensor.transpose(out=sm_t[:, h, :], in_=sm_h[:, h, :], identity=ident[:])
-        for u in range(2):
-            nc.tensor.transpose(out=sm_t[:, 2 + u, :], in_=sm[:, u : 2 * P : 2], identity=ident[:])
-        sm_s = const.tile([P, 4, P], F32, name="sm_s")
-        nc.vector.tensor_copy(out=sm_s[:], in_=sm_t[:])
-        sm_v = sm_s[:].bitcast(BF16).rearrange("p k (row e) -> p k row e", e=2)
-        bias_f = const.tile([P, O, 4], F32, name="bias_f")
-        bias_v = bias_f[:].rearrange("p o (u e) -> p u o e", u=2)
-        for u in range(2):
-            nc.vector.tensor_copy(out=bias_v[:, u], in_=sm_v[:, 2 + u, 64:66, :])
+        nc.scalar.activation(out=warm_o[:], in_=warm[:], func=ACT.Exp, bias=0.0, scale=1.0)
 
         w_q = const.tile([P, O * D], U32, name="w_q", align_bytes=64)
         w_s = const.tile([P, O * D], U8, name="w_s", align_bytes=64)
@@ -119,11 +105,12 @@ def tile_biaffine_pa_t_kernel(tc, x1, x2, bw, W_bil, t_ones, lin1, lin2, b_lin, 
                     out=dst[:, uj], in0=src[:, uj], scalar1=1.0, scalar2=0.0, op0=ALU.mult, op1=ALU.add
                 )
 
-        def quant_w(o):
+        def quant_w(o, uj):
+            c0 = o * D + uj * 256
             nc.vector.quantize_mx(
-                out=w_q[:, o * D : (o + 1) * D].bitcast(FP8X4),
-                scales=w_s[:, o * D : (o + 1) * D],
-                in_=w_g[o][:],
+                out=w_q[:, c0 : c0 + 256].bitcast(FP8X4),
+                scales=w_s[:, c0 : c0 + 256],
+                in_=w_g[o][:, uj * 1024 : uj * 1024 + 1024],
             )
 
         pt_x = {}
@@ -136,64 +123,56 @@ def tile_biaffine_pa_t_kernel(tc, x1, x2, bw, W_bil, t_ones, lin1, lin2, b_lin, 
         pp = {}
         tp = {}
         st = {}
+        sp = {}
 
-        def transposes(b):
-            for which, store in ((0, x1_raw), (1, x2_raw)):
-                xr, k = store[b]
-                words = xr[:].bitcast(F32)
-                pt = ps_t.tile([P, H, 2, P], F32, name="pt", tag="pt")
-                for h in range(H):
-                    for u in range(2):
-                        c0 = h * 256
-                        nc.tensor.transpose(
-                            out=pt[:, h, u, :], in_=words[:, k, c0 + u : c0 + 256 : 2], identity=ident[:]
-                        )
-                pt_x[(b, which)] = pt
+        def transposes(b, which):
+            xr, k = (x1_raw, x2_raw)[which][b]
+            words = xr[:].bitcast(F32)
+            pt = ps_t.tile([P, H, 2, P], F32, name="pt", tag="pt")
+            for h in range(H):
+                for u in range(2):
+                    c0 = h * 256
+                    nc.tensor.transpose(
+                        out=pt[:, h, u, :], in_=words[:, k, c0 + u : c0 + 256 : 2], identity=ident[:]
+                    )
+            pt_x[(b, which)] = pt
 
-        def exit_x1(b):
-            x1g = stage.tile([P, 4 * L], BF16, name="x1g", align_bytes=64)
-            nc.scalar.copy(
-                out=x1g[:].bitcast(F32).rearrange("q (h r u) -> q h r u", h=H, u=2),
-                in_=pt_x[(b, 0)][:].rearrange("q h u r -> q h r u"),
-            )
-            xg[(b, 0)] = x1g
+        def exit_x(b, which):
+            g = stage.tile([P, 4 * L], BF16, name="x%dg" % which, align_bytes=64)
+            if which == 0:
+                dst = g[:].bitcast(F32).rearrange("q (h r u) -> q h r u", h=H, u=2)
+            else:
+                dst = g[:].bitcast(F32).rearrange("q (r h u) -> q h r u", h=H, u=2)
+            if which == 0:
+                nc.scalar.copy(out=dst, in_=pt_x[(b, which)][:].rearrange("q h u r -> q h r u"))
+            else:
+                nc.scalar.copy(
+                    out=g[:].bitcast(F32).rearrange("q (r h u) -> q r h u", h=H, u=2),
+                    in_=pt_x[(b, which)][:].rearrange("q h u r -> q r h u"),
+                )
+            xg[(b, which)] = g
 
-        def exit_x2(b):
-            x2g = stage.tile([P, 4 * L], BF16, name="x2g", align_bytes=64)
-            nc.scalar.copy(
-                out=x2g[:].bitcast(F32).rearrange("q (r h u) -> q r h u", h=H, u=2),
-                in_=pt_x[(b, 1)][:].rearrange("q h u r -> q r h u"),
-            )
-            xg[(b, 1)] = x2g
+        def quant_x(b, which):
+            pool = (keep3, keep4)[which]
+            q = pool.tile([P, L], U32, name="x%dq" % which, align_bytes=64)
+            s = pool.tile([P, L], U8, name="x%ds" % which, align_bytes=64)
+            nc.vector.quantize_mx(out=q[:].bitcast(FP8X4), scales=s[:], in_=xg[(b, which)][:])
+            xq[(b, which)] = (q, s)
 
-        def quant_x1(b):
-            x1q = keep3.tile([P, L], U32, name="x1q", align_bytes=64)
-            x1s = keep3.tile([P, L], U8, name="x1s", align_bytes=64)
-            nc.vector.quantize_mx(out=x1q[:].bitcast(FP8X4), scales=x1s[:], in_=xg[(b, 0)][:])
-            xq[(b, 0)] = (x1q, x1s)
-
-        def quant_x2(b):
-            x2q = keep4.tile([P, L], U32, name="x2q", align_bytes=64)
-            x2s = keep4.tile([P, L], U8, name="x2s", align_bytes=64)
-            nc.vector.quantize_mx(out=x2q[:].bitcast(FP8X4), scales=x2s[:], in_=xg[(b, 1)][:])
-            xq[(b, 1)] = (x2q, x2s)
-
-        def stage1(b, g):
-            o, h = g // H, g % H
+        def stage1(b, h):
             x1q, x1s = xq[(b, 0)]
             acc = ps_1.tile([P, 4, P], F32, name="p1", tag="p1")
             for c in range(4):
-                w0 = (o * 4 + c) * P
                 nc.tensor.matmul_mx(
                     out=acc[:, c, :],
-                    lhsT=w_q[:, w0 : w0 + P].bitcast(FP8X4),
-                    lhsT_scale=w_s[:, w0 : w0 + P],
+                    lhsT=w_q[:, c * P : c * P + P].bitcast(FP8X4),
+                    lhsT_scale=w_s[:, c * P : c * P + P],
                     rhs=x1q[:, h * P : (h + 1) * P].bitcast(FP8X4),
                     rhs_scale=x1s[:, h * P : (h + 1) * P],
                     start=True,
                     stop=True,
                 )
-            p1[(b, g)] = acc
+            p1[(b, h)] = acc
 
         def get_tg(b):
             if b not in tg:
@@ -201,13 +180,12 @@ def tile_biaffine_pa_t_kernel(tc, x1, x2, bw, W_bil, t_ones, lin1, lin2, b_lin, 
                 tg[b] = tgt
             return tg[b]
 
-        def t_out(b, g):
-            o = g // H
+        def t_out(b, h):
             view = get_tg(b)[:].rearrange("q (g r c) -> q g r c", g=O * H, c=4)
             nc.vector.tensor_tensor(
-                out=view[:, g],
-                in0=p1[(b, g)][:].rearrange("q c r -> q r c"),
-                in1=bias_f[:, o, :].unsqueeze(1).to_broadcast([P, P, 4]),
+                out=view[:, h],
+                in0=p1[(b, h)][:].rearrange("q c r -> q r c"),
+                in1=bias_f[:, 0, :].unsqueeze(1).to_broadcast([P, P, 4]),
                 op=ALU.add,
             )
 
@@ -235,22 +213,21 @@ def tile_biaffine_pa_t_kernel(tc, x1, x2, bw, W_bil, t_ones, lin1, lin2, b_lin, 
                     )
                 p2[(b, h)] = acc
 
-        def planar_pe(b):
+        def planar_pe(b, cp):
             x1q, x1s = xq[(b, 0)]
-            for cp in range(2):
-                acc = ps_t.tile([P, 2, L], F32, name="pt", tag="pt")
-                for ci in range(2):
-                    w0 = (4 + 2 * cp + ci) * P
-                    nc.tensor.matmul_mx(
-                        out=acc[:, ci, :],
-                        lhsT=w_q[:, w0 : w0 + P].bitcast(FP8X4),
-                        lhsT_scale=w_s[:, w0 : w0 + P],
-                        rhs=x1q[:].bitcast(FP8X4),
-                        rhs_scale=x1s[:],
-                        start=True,
-                        stop=True,
-                    )
-                pp[(b, cp)] = acc
+            acc = ps_t.tile([P, 2, L], F32, name="pt", tag="pt")
+            for ci in range(2):
+                w0 = (4 + 2 * cp + ci) * P
+                nc.tensor.matmul_mx(
+                    out=acc[:, ci, :],
+                    lhsT=w_q[:, w0 : w0 + P].bitcast(FP8X4),
+                    lhsT_scale=w_s[:, w0 : w0 + P],
+                    rhs=x1q[:].bitcast(FP8X4),
+                    rhs_scale=x1s[:],
+                    start=True,
+                    stop=True,
+                )
+            pp[(b, cp)] = acc
 
         def planar_exits(b):
             tpt = stage.tile([P, 4, L], BF16, name="tp")
@@ -265,24 +242,19 @@ def tile_biaffine_pa_t_kernel(tc, x1, x2, bw, W_bil, t_ones, lin1, lin2, b_lin, 
             tp[b] = tpt
 
         def regroup_t(b):
-            dst = get_tg(b)[:, 4 * L : 8 * L].rearrange("q (xb i t) -> q xb t i", i=4, t=4)
-            src = tp[b][:].rearrange("q t (xb i) -> q xb t i", i=4)
-            if REGROUP_ENGINE == "vector":
-                nc.vector.tensor_copy(out=dst, in_=src)
-            else:
-                dst = get_tg(b)[:, 4 * L : 8 * L].rearrange("q (x t) -> q x t", t=4)
-                src = tp[b][:].rearrange("q t x -> q x t")
-                for k in range(2):
-                    nc.gpsimd.tensor_scalar(
-                        out=dst[:, P * k : P * k + P],
-                        in0=src[:, P * k : P * k + P],
-                        scalar1=1.0,
-                        scalar2=0.0,
-                        op0=ALU.mult,
-                        op1=ALU.add,
-                    )
+            dst = get_tg(b)[:, 4 * L : 8 * L].rearrange("q (x t) -> q x t", t=4)
+            src = tp[b][:].rearrange("q t x -> q x t")
+            for k in range(2):
+                nc.gpsimd.tensor_scalar(
+                    out=dst[:, P * k : P * k + P],
+                    in0=src[:, P * k : P * k + P],
+                    scalar1=1.0,
+                    scalar2=0.0,
+                    op0=ALU.mult,
+                    op1=ALU.add,
+                )
 
-        def spread_lin2(b):
+        def spread(b):
             acc = ps_t.tile([P, L, O], F32, name="pt", tag="pt")
             nc.tensor.matmul(
                 out=acc[:].rearrange("p y o -> p (y o)"),
@@ -291,12 +263,15 @@ def tile_biaffine_pa_t_kernel(tc, x1, x2, bw, W_bil, t_ones, lin1, lin2, b_lin, 
                 start=True,
                 stop=True,
             )
+            sp[b] = acc
+
+        def add_x_terms(b):
             stt = keep3.tile([P, H, O, L], F32, name="st")
             for h in range(H):
                 for o in range(O):
                     nc.scalar.activation(
                         out=stt[:, h, o, :],
-                        in_=acc[:, :, o],
+                        in_=sp[b][:, :, o],
                         func=ACT.Identity,
                         bias=a_x[:, h, b, o : o + 1],
                         scale=bwn[:, 1:2],
@@ -325,11 +300,42 @@ def tile_biaffine_pa_t_kernel(tc, x1, x2, bw, W_bil, t_ones, lin1, lin2, b_lin, 
                     in_=ot[:].rearrange("p h y o -> p (h y o)"),
                 )
 
-        def softmax_tail():
+        bwf = const.tile([P, 2], F32, name="bwf")
+        negm = const.tile([P, 1], F32, name="negm")
+        ebw = const.tile([P, 2], F32, name="ebw")
+        esum = const.tile([P, 1], F32, name="esum")
+        rsum = const.tile([P, 1], F32, name="rsum")
+        bwn = const.tile([P, 2], F32, name="bwn")
+        blf = const.tile([P, 2], F32, name="blf")
+        a_x = const.tile([P, H, B, O], F32, name="a_x")
+        bias_f = const.tile([P, O, 4], F32, name="bias_f")
+        sm_s = const.tile([P, H, P], F32, name="sm_s")
+
+        def softmax_1():
+            nc.vector.tensor_copy(out=bwf[:], in_=bw_b[:])
+            nc.vector.tensor_tensor(out=negm[:], in0=bwf[:, 0:1], in1=bwf[:, 1:2], op=ALU.max)
+            nc.vector.tensor_scalar_mul(out=negm[:], in0=negm[:], scalar1=-1.0)
+
+        def softmax_2():
+            nc.scalar.activation(out=ebw[:], in_=bwf[:], func=ACT.Exp, bias=negm[:], scale=1.0)
+
+        def small_pe():
+            sm_t = ps_t.tile([P, H, P], F32, name="pt", tag="pt")
+            sm_h = sm[:].rearrange("p (r h) -> p h r", h=H)
+            for h in range(H):
+                nc.tensor.transpose(out=sm_t[:, h, :], in_=sm_h[:, h, :], identity=ident[:])
+            return sm_t
+
+        def copy_small(sm_t):
+            nc.vector.tensor_copy(out=sm_s[:], in_=sm_t[:])
+
+        def softmax_3():
             nc.vector.tensor_tensor(out=esum[:], in0=ebw[:, 0:1], in1=ebw[:, 1:2], op=ALU.add)
-            nc.vector.reciprocal(out=rsum[:], in_=esum[:])
-            nc.vector.tensor_scalar_mul(out=bwn[:], in0=ebw[:], scalar1=rsum[:])
             nc.vector.tensor_copy(out=blf[:], in_=bl_b[:])
+
+        def softmax_4():
+            sm_v = sm_s[:].bitcast(BF16).rearrange("p k (row e) -> p k row e", e=2)
+            nc.vector.reciprocal(out=rsum[:], in_=esum[:])
             for h in range(H):
                 nc.vector.tensor_tensor(
                     out=a_x[:, h],
@@ -337,8 +343,16 @@ def tile_biaffine_pa_t_kernel(tc, x1, x2, bw, W_bil, t_ones, lin1, lin2, b_lin, 
                     in1=blf[:].unsqueeze(1).to_broadcast([P, B, O]),
                     op=ALU.add,
                 )
+
+        def softmax_5():
+            nc.vector.tensor_scalar_mul(out=bwn[:], in0=ebw[:], scalar1=rsum[:])
+
+        def softmax_6():
             a_flat = a_x[:].rearrange("p h b o -> p (h b o)")
             nc.vector.tensor_scalar_mul(out=a_flat, in0=a_flat, scalar1=bwn[:, 1:2])
+
+        def softmax_7():
+            sm_v = sm_s[:].bitcast(BF16).rearrange("p k (row e) -> p k row e", e=2)
             for h in range(H):
                 nc.vector.scalar_tensor_tensor(
                     out=a_x[:, h],
@@ -349,74 +363,75 @@ def tile_biaffine_pa_t_kernel(tc, x1, x2, bw, W_bil, t_ones, lin1, lin2, b_lin, 
                     op1=ALU.add,
                 )
 
-        esum = const.tile([P, 1], F32, name="esum")
-        rsum = const.tile([P, 1], F32, name="rsum")
-        bwn = const.tile([P, 2], F32, name="bwn")
-        blf = const.tile([P, 2], F32, name="blf")
-        a_x = const.tile([P, H, B, O], F32, name="a_x")
-
+        transposes(0, 0)
+        exit_x(0, 0)
         regroup_w(0, 0, "vector")
-        regroup_w(0, 1, "vector")
-        transposes(0)
-        exit_x1(0)
-        regroup_w(1, 0, "scalar")
-        regroup_w(1, 1, "gpsimd")
-        exit_x2(0)
-        quant_w(0)
-        quant_x1(0)
+        nc.vector.tensor_copy(out=bias_f[:], in_=bias_b[:])
+        regroup_w(0, 1, "scalar")
+        quant_x(0, 0)
+        quant_w(0, 0)
+        sm_t = small_pe()
+        transposes(0, 1)
+        regroup_w(1, 0, "vector")
+        softmax_1()
+        exit_x(0, 1)
+        quant_w(0, 1)
+        copy_small(sm_t)
+        softmax_2()
+        regroup_w(1, 1, "scalar")
         stage1(0, 0)
         stage1(0, 1)
-        transposes(1)
-        exit_x1(1)
-        exit_x2(1)
-
+        transposes(1, 0)
+        quant_w(1, 0)
         t_out(0, 0)
+        softmax_3()
         t_out(0, 1)
-        quant_w(1)
-        quant_x2(0)
-        quant_x1(1)
-        quant_x2(1)
-        softmax_tail()
-        planar_pe(0)
+        softmax_4()
+        transposes(1, 1)
+        exit_x(1, 0)
+        exit_x(1, 1)
+        quant_w(1, 1)
+        softmax_5()
+        planar_pe(0, 0)
+        planar_pe(0, 1)
+        quant_x(0, 1)
+        softmax_6()
+        quant_x(1, 0)
+        softmax_7()
+        quant_x(1, 1)
         planar_exits(0)
         regroup_t(0)
-        transposes(2)
-        exit_x1(2)
-        exit_x2(2)
-        planar_pe(1)
-        stage1(1, 0)
-        stage1(1, 1)
-        planar_exits(1)
-        regroup_t(1)
-        spread_lin2(0)
-        spread_lin2(1)
-        quant_x1(2)
-        quant_x2(2)
-        quant_t(0)
-        transposes(3)
+        transposes(2, 0)
+        transposes(2, 1)
 
-        for b in range(1, B + 1):
-            stage2(b - 1)
-            if b + 2 < B:
-                exit_x1(b + 2)
-                exit_x2(b + 2)
-            if b + 1 < B:
-                planar_pe(b + 1)
-            if b < B:
-                for g in range(H):
-                    t_out(b, g)
-                    if b + 1 < B:
-                        stage1(b + 1, g)
-            if b + 1 < B:
-                planar_exits(b + 1)
-                regroup_t(b + 1)
-            out_exit(b - 1)
-            if b + 1 < B:
-                spread_lin2(b + 1)
-            if b + 2 < B:
-                quant_x1(b + 2)
-                quant_x2(b + 2)
-            if b < B:
-                quant_t(b)
-            if b + 3 < B:
-                transposes(b + 3)
+        for k in range(B + 1):
+            if k < B:
+                spread(k)
+            if k > 0:
+                stage2(k - 1)
+            if k + 2 < B:
+                exit_x(k + 2, 0)
+                exit_x(k + 2, 1)
+            if k + 1 < B:
+                planar_pe(k + 1, 0)
+                planar_pe(k + 1, 1)
+            for h in range(H):
+                if 0 < k < B:
+                    t_out(k, h)
+                if k + 1 < B:
+                    stage1(k + 1, h)
+            if k < B:
+                add_x_terms(k)
+            if k > 0:
+                out_exit(k - 1)
+            if k < B:
+                quant_t(k)
+            if k + 1 < B:
+                planar_exits(k + 1)
+                regroup_t(k + 1)
+            if k + 2 < B:
+                quant_x(k + 2, 0)
+                quant_x(k + 2, 1)
+            if k + 3 < B:
+                transposes(k + 3, 0)
+                transposes(k + 3, 1)

@@ -36,7 +36,7 @@ def tile_biaffine_pa_t_kernel(tc, x1, x2, bw, W_bil, t_ones, lin1, lin2, b_lin, 
         nc.vector.memset(warm[:], 0.0)
         warm_o = const.tile([P, 1], F32, name="warm_o")
         sm = const.tile([P, 256], F32, name="sm")
-        nc.vector.memset(sm[:], 0.0)
+        nc.gpsimd.memset(sm[:], 0.0)
         l2r = const.tile([P, L * O], BF16, name="l2r")
         nc.vector.memset(l2r[:], 0.0)
         ident = const.tile([P, P], F32, name="ident")
@@ -72,19 +72,19 @@ def tile_biaffine_pa_t_kernel(tc, x1, x2, bw, W_bil, t_ones, lin1, lin2, b_lin, 
         load_w(0)
         load_w(1)
         nc.sync.dma_start(out=bias_b[:], in_=W_bil[:, D, :].rearrange("o (p c) -> p o c", c=4))
+        load_x(x2, x2_raw, "x2", 0, 1)
+        load_x(x1, x1_raw, "x1", 1, 1)
         nc.sync.dma_start(out=bw_b[:], in_=bw.partition_broadcast(P))
+        load_x(x2, x2_raw, "x2", 1, 1)
         nc.sync.dma_start(out=sm_bf[0:16, :], in_=t_ones.rearrange("b x o -> b (x o)"))
         nc.sync.dma_start(out=sm_bf[32:48, :], in_=lin1.rearrange("b x o -> b (x o)"))
-        load_x(x2, x2_raw, "x2", 0, 1)
         nc.sync.dma_start(out=bl_b[:], in_=b_lin.partition_broadcast(P))
         nc.sync.dma_start(out=l2r[0:B, :], in_=lin2.rearrange("b y o -> b (y o)"))
-        load_x(x1, x1_raw, "x1", 1, 1)
-        load_x(x2, x2_raw, "x2", 1, 1)
         for b0, nb in LOAD_GROUPS[1:]:
             load_x(x1, x1_raw, "x1", b0, nb)
             load_x(x2, x2_raw, "x2", b0, nb)
 
-        nc.scalar.activation(out=warm_o[:], in_=warm[:], func=ACT.Exp, bias=0.0, scale=1.0)
+        nc.scalar.activation(out=warm_o[:], in_=warm[:], func=ACT.Sigmoid, bias=0.0, scale=1.0)
 
         w_q = const.tile([P, O * D], U32, name="w_q", align_bytes=64)
         w_s = const.tile([P, O * D], U8, name="w_s", align_bytes=64)
@@ -124,6 +124,7 @@ def tile_biaffine_pa_t_kernel(tc, x1, x2, bw, W_bil, t_ones, lin1, lin2, b_lin, 
         tp = {}
         st = {}
         sp = {}
+        ots = {}
 
         def transposes(b, which):
             xr, k = (x1_raw, x2_raw)[which][b]
@@ -159,20 +160,22 @@ def tile_biaffine_pa_t_kernel(tc, x1, x2, bw, W_bil, t_ones, lin1, lin2, b_lin, 
             nc.vector.quantize_mx(out=q[:].bitcast(FP8X4), scales=s[:], in_=xg[(b, which)][:])
             xq[(b, which)] = (q, s)
 
-        def stage1(b, h):
+        def stage1(b, g):
+            o, h = g // H, g % H
             x1q, x1s = xq[(b, 0)]
             acc = ps_1.tile([P, 4, P], F32, name="p1", tag="p1")
             for c in range(4):
+                w0 = (o * 4 + c) * P
                 nc.tensor.matmul_mx(
                     out=acc[:, c, :],
-                    lhsT=w_q[:, c * P : c * P + P].bitcast(FP8X4),
-                    lhsT_scale=w_s[:, c * P : c * P + P],
+                    lhsT=w_q[:, w0 : w0 + P].bitcast(FP8X4),
+                    lhsT_scale=w_s[:, w0 : w0 + P],
                     rhs=x1q[:, h * P : (h + 1) * P].bitcast(FP8X4),
                     rhs_scale=x1s[:, h * P : (h + 1) * P],
                     start=True,
                     stop=True,
                 )
-            p1[(b, h)] = acc
+            p1[(b, g)] = acc
 
         def get_tg(b):
             if b not in tg:
@@ -180,28 +183,37 @@ def tile_biaffine_pa_t_kernel(tc, x1, x2, bw, W_bil, t_ones, lin1, lin2, b_lin, 
                 tg[b] = tgt
             return tg[b]
 
-        def t_out(b, h):
-            view = get_tg(b)[:].rearrange("q (g r c) -> q g r c", g=O * H, c=4)
+        def t_out(b, g):
+            o, h = g // H, g % H
+            view = get_tg(b)[:].rearrange("q (h o r c) -> q h o r c", h=H, o=O, c=4)
             nc.vector.tensor_tensor(
-                out=view[:, h],
-                in0=p1[(b, h)][:].rearrange("q c r -> q r c"),
-                in1=bias_f[:, 0, :].unsqueeze(1).to_broadcast([P, P, 4]),
+                out=view[:, h, o],
+                in0=p1[(b, g)][:].rearrange("q c r -> q r c"),
+                in1=bias_f[:, o, :].unsqueeze(1).to_broadcast([P, P, 4]),
                 op=ALU.add,
             )
 
-        def quant_t(b):
-            tqt = stage.tile([P, O * L], U32, name="tq", align_bytes=64)
-            tst = stage.tile([P, O * L], U8, name="ts", align_bytes=64)
-            nc.vector.quantize_mx(out=tqt[:].bitcast(FP8X4), scales=tst[:], in_=tg[b][:])
-            tq[b] = (tqt, tst)
+        def quant_t(b, h0, nh):
+            if b not in tq:
+                tqt = stage.tile([P, O * L], U32, name="tq", align_bytes=64)
+                tst = stage.tile([P, O * L], U8, name="ts", align_bytes=64)
+                tq[b] = (tqt, tst)
+            tqt, tst = tq[b]
+            c0, c1 = h0 * L, (h0 + nh) * L
+            nc.vector.quantize_mx(
+                out=tqt[:, c0:c1].bitcast(FP8X4), scales=tst[:, c0:c1], in_=tg[b][:, 4 * c0 : 4 * c1]
+            )
 
-        def stage2(b):
+        def stage2(b, halves):
             tqt, tst = tq[b]
             x2q, x2s = xq[(b, 1)]
-            for h in range(H):
-                acc = ps_2.tile([P, O, L], F32, name="p2", tag="p2")
+            for h in halves:
+                if b == B - 1:
+                    acc = ps_t.tile([P, O, L], F32, name="pt", tag="pt")
+                else:
+                    acc = ps_2.tile([P, O, L], F32, name="p2", tag="p2")
                 for o in range(O):
-                    c0 = (o * H + h) * P
+                    c0 = (h * O + o) * P
                     nc.tensor.matmul_mx(
                         out=acc[:, o, :],
                         lhsT=tqt[:, c0 : c0 + P].bitcast(FP8X4),
@@ -241,13 +253,34 @@ def tile_biaffine_pa_t_kernel(tc, x1, x2, bw, W_bil, t_ones, lin1, lin2, b_lin, 
                 )
             tp[b] = tpt
 
+        def t_out_scalar(b, g):
+            tpt = stage.tile([P, 4, P], BF16, name="tp1")
+            for c in range(4):
+                nc.scalar.activation(
+                    out=tpt[:, c, :],
+                    in_=p1[(b, g)][:, c, :],
+                    func=ACT.Identity,
+                    bias=bias_f[:, g // H, c : c + 1],
+                    scale=1.0,
+                )
+            o, h = g // H, g % H
+            dst = get_tg(b)[:].rearrange("q (h o r t) -> q h o r t", h=H, o=O, t=4)
+            nc.gpsimd.tensor_scalar(
+                out=dst[:, h, o],
+                in0=tpt[:].rearrange("q t r -> q r t"),
+                scalar1=1.0,
+                scalar2=0.0,
+                op0=ALU.mult,
+                op1=ALU.add,
+            )
+
         def regroup_t(b):
-            dst = get_tg(b)[:, 4 * L : 8 * L].rearrange("q (x t) -> q x t", t=4)
-            src = tp[b][:].rearrange("q t x -> q x t")
-            for k in range(2):
+            dst = get_tg(b)[:].rearrange("q (h o r t) -> q h o r t", h=H, o=O, t=4)
+            src = tp[b][:].rearrange("q t (h r) -> q h r t", h=H)
+            for h in range(H):
                 nc.gpsimd.tensor_scalar(
-                    out=dst[:, P * k : P * k + P],
-                    in0=src[:, P * k : P * k + P],
+                    out=dst[:, h, 1],
+                    in0=src[:, h],
                     scalar1=1.0,
                     scalar2=0.0,
                     op0=ALU.mult,
@@ -278,9 +311,12 @@ def tile_biaffine_pa_t_kernel(tc, x1, x2, bw, W_bil, t_ones, lin1, lin2, b_lin, 
                     )
             st[b] = stt
 
-        def out_exit(b):
-            ot = keep4.tile([P, H, L, O], F32, name="ot")
-            for h in range(H):
+        def out_exit(b, halves):
+            if b not in ots:
+                ott = keep4.tile([P, H, L, O], F32, name="ot")
+                ots[b] = ott
+            ot = ots[b]
+            for h in halves:
                 nc.vector.scalar_tensor_tensor(
                     out=ot[:, h],
                     in0=p2[(b, h)][:].rearrange("p o y -> p y o"),
@@ -289,35 +325,28 @@ def tile_biaffine_pa_t_kernel(tc, x1, x2, bw, W_bil, t_ones, lin1, lin2, b_lin, 
                     op0=ALU.mult,
                     op1=ALU.add,
                 )
-                if b == B - 1:
+                if b >= B - 3:
                     nc.sync.dma_start(
                         out=out[b].rearrange("(p h) y o -> p h (y o)", h=H)[:, h, :],
                         in_=ot[:, h].rearrange("p y o -> p (y o)"),
                     )
-            if b < B - 1:
+            if b < B - 3:
                 nc.sync.dma_start(
                     out=out[b].rearrange("(p h) y o -> p (h y o)", h=H),
                     in_=ot[:].rearrange("p h y o -> p (h y o)"),
                 )
 
-        bwf = const.tile([P, 2], F32, name="bwf")
-        negm = const.tile([P, 1], F32, name="negm")
-        ebw = const.tile([P, 2], F32, name="ebw")
-        esum = const.tile([P, 1], F32, name="esum")
-        rsum = const.tile([P, 1], F32, name="rsum")
+        dif = const.tile([P, 1], F32, name="dif")
         bwn = const.tile([P, 2], F32, name="bwn")
-        blf = const.tile([P, 2], F32, name="blf")
+        a_l = const.tile([P, H, B, O], F32, name="a_l")
         a_x = const.tile([P, H, B, O], F32, name="a_x")
         bias_f = const.tile([P, O, 4], F32, name="bias_f")
         sm_s = const.tile([P, H, P], F32, name="sm_s")
 
-        def softmax_1():
-            nc.vector.tensor_copy(out=bwf[:], in_=bw_b[:])
-            nc.vector.tensor_tensor(out=negm[:], in0=bwf[:, 0:1], in1=bwf[:, 1:2], op=ALU.max)
-            nc.vector.tensor_scalar_mul(out=negm[:], in0=negm[:], scalar1=-1.0)
-
-        def softmax_2():
-            nc.scalar.activation(out=ebw[:], in_=bwf[:], func=ACT.Exp, bias=negm[:], scale=1.0)
+        def mix_weights():
+            nc.gpsimd.tensor_tensor(out=dif[:], in0=bw_b[:, 1:2], in1=bw_b[:, 0:1], op=ALU.subtract)
+            nc.scalar.activation(out=bwn[:, 0:1], in_=dif[:], func=ACT.Sigmoid, bias=0.0, scale=-1.0)
+            nc.scalar.activation(out=bwn[:, 1:2], in_=dif[:], func=ACT.Sigmoid, bias=0.0, scale=1.0)
 
         def small_pe():
             sm_t = ps_t.tile([P, H, P], F32, name="pt", tag="pt")
@@ -327,111 +356,114 @@ def tile_biaffine_pa_t_kernel(tc, x1, x2, bw, W_bil, t_ones, lin1, lin2, b_lin, 
             return sm_t
 
         def copy_small(sm_t):
-            nc.vector.tensor_copy(out=sm_s[:], in_=sm_t[:])
+            nc.scalar.copy(out=sm_s[:], in_=sm_t[:])
 
-        def softmax_3():
-            nc.vector.tensor_tensor(out=esum[:], in0=ebw[:, 0:1], in1=ebw[:, 1:2], op=ALU.add)
-            nc.vector.tensor_copy(out=blf[:], in_=bl_b[:])
-
-        def softmax_4():
+        def x_terms():
             sm_v = sm_s[:].bitcast(BF16).rearrange("p k (row e) -> p k row e", e=2)
-            nc.vector.reciprocal(out=rsum[:], in_=esum[:])
             for h in range(H):
-                nc.vector.tensor_tensor(
-                    out=a_x[:, h],
+                nc.gpsimd.tensor_tensor(
+                    out=a_l[:, h],
                     in0=sm_v[:, h, 32:48, :],
-                    in1=blf[:].unsqueeze(1).to_broadcast([P, B, O]),
+                    in1=bl_b[:].unsqueeze(1).to_broadcast([P, B, O]),
                     op=ALU.add,
                 )
-
-        def softmax_5():
-            nc.vector.tensor_scalar_mul(out=bwn[:], in0=ebw[:], scalar1=rsum[:])
-
-        def softmax_6():
-            a_flat = a_x[:].rearrange("p h b o -> p (h b o)")
-            nc.vector.tensor_scalar_mul(out=a_flat, in0=a_flat, scalar1=bwn[:, 1:2])
-
-        def softmax_7():
-            sm_v = sm_s[:].bitcast(BF16).rearrange("p k (row e) -> p k row e", e=2)
-            for h in range(H):
-                nc.vector.scalar_tensor_tensor(
+                nc.gpsimd.tensor_scalar(
                     out=a_x[:, h],
                     in0=sm_v[:, h, 0:16, :],
-                    scalar=bwn[:, 0:1],
-                    in1=a_x[:, h],
+                    scalar1=bwn[:, 0:1],
+                    scalar2=0.0,
                     op0=ALU.mult,
                     op1=ALU.add,
                 )
+            al_flat = a_l[:].rearrange("p h b o -> p (h b o)")
+            ax_flat = a_x[:].rearrange("p h b o -> p (h b o)")
+            nc.gpsimd.tensor_scalar(
+                out=al_flat, in0=al_flat, scalar1=bwn[:, 1:2], scalar2=0.0, op0=ALU.mult, op1=ALU.add
+            )
+            nc.gpsimd.tensor_tensor(out=ax_flat, in0=ax_flat, in1=al_flat, op=ALU.add)
 
         transposes(0, 0)
         exit_x(0, 0)
         regroup_w(0, 0, "vector")
-        nc.vector.tensor_copy(out=bias_f[:], in_=bias_b[:])
-        regroup_w(0, 1, "scalar")
+        regroup_w(0, 1, "vector")
+        regroup_w(1, 0, "scalar")
         quant_x(0, 0)
         quant_w(0, 0)
-        sm_t = small_pe()
-        transposes(0, 1)
-        regroup_w(1, 0, "vector")
-        softmax_1()
-        exit_x(0, 1)
         quant_w(0, 1)
-        copy_small(sm_t)
-        softmax_2()
-        regroup_w(1, 1, "scalar")
+        nc.gpsimd.tensor_copy(out=bias_f[:], in_=bias_b[:])
+        mix_weights()
+        transposes(0, 1)
         stage1(0, 0)
         stage1(0, 1)
-        transposes(1, 0)
-        quant_w(1, 0)
+        regroup_w(1, 1, "scalar")
         t_out(0, 0)
-        softmax_3()
+        sm_t = small_pe()
+        transposes(1, 0)
+        exit_x(0, 1)
+        copy_small(sm_t)
+        x_terms()
         t_out(0, 1)
-        softmax_4()
-        transposes(1, 1)
-        exit_x(1, 0)
-        exit_x(1, 1)
+        quant_w(1, 0)
         quant_w(1, 1)
-        softmax_5()
-        planar_pe(0, 0)
-        planar_pe(0, 1)
+        stage1(0, 2)
+        stage1(0, 3)
+        exit_x(1, 0)
         quant_x(0, 1)
-        softmax_6()
+        t_out(0, 2)
+        transposes(1, 1)
+        exit_x(1, 1)
         quant_x(1, 0)
-        softmax_7()
+        t_out(0, 3)
         quant_x(1, 1)
-        planar_exits(0)
-        regroup_t(0)
         transposes(2, 0)
         transposes(2, 1)
 
-        for k in range(B + 1):
-            if k < B:
-                spread(k)
+        for k in range(B):
+            if k > 1:
+                stage2(k - 1, range(H))
             if k > 0:
-                stage2(k - 1)
+                spread(k)
             if k + 2 < B:
                 exit_x(k + 2, 0)
                 exit_x(k + 2, 1)
             if k + 1 < B:
                 planar_pe(k + 1, 0)
                 planar_pe(k + 1, 1)
+            if k == 0:
+                spread(k)
             for h in range(H):
-                if 0 < k < B:
+                if 0 < k < B - 1 or (k == B - 1 and h == 0):
                     t_out(k, h)
                 if k + 1 < B:
                     stage1(k + 1, h)
-            if k < B:
-                add_x_terms(k)
-            if k > 0:
-                out_exit(k - 1)
-            if k < B:
-                quant_t(k)
-            if k + 1 < B:
+                if k == B - 1:
+                    out_exit(k - 1, [h])
+                    quant_t(k, h, 1)
+            if k == 0 or k == B - 2:
+                planar_exits(k + 1)
+                regroup_t(k + 1)
+            if k == B - 2:
+                t_out_scalar(k + 1, 1)
+            add_x_terms(k)
+            if k < B - 2:
+                if k > 0:
+                    out_exit(k - 1, range(H))
+                quant_t(k, 0, H)
+            elif k == B - 2:
+                out_exit(k - 1, [0])
+                quant_t(k, 0, H)
+                out_exit(k - 1, [1])
+            if 0 < k < B - 2:
                 planar_exits(k + 1)
                 regroup_t(k + 1)
             if k + 2 < B:
                 quant_x(k + 2, 0)
                 quant_x(k + 2, 1)
+            if k == 0:
+                stage2(0, range(H))
             if k + 3 < B:
                 transposes(k + 3, 0)
                 transposes(k + 3, 1)
+        for h in range(H):
+            stage2(B - 1, [h])
+            out_exit(B - 1, [h])

@@ -36,13 +36,12 @@ def tile_biaffine_pa_t_kernel(tc, x1, x2, bw, W_bil, t_ones, lin1, lin2, b_lin, 
         nc.vector.memset(warm[:], 0.0)
         warm_o = const.tile([P, 1], F32, name="warm_o")
         sm = const.tile([P, 256], F32, name="sm")
-        nc.gpsimd.memset(sm[:], 0.0)
-        l2r = const.tile([P, L * O], BF16, name="l2r")
-        nc.vector.memset(l2r[:], 0.0)
+        nc.vector.memset(sm[:], 0.0)
+        l2w = const.tile([P, L], F32, name="l2w")
+        nc.vector.memset(l2w[:], 0.0)
+        l2t = const.tile([P, 2, B], F32, name="l2t")
         ident = const.tile([P, P], F32, name="ident")
         make_identity(nc, ident[:])
-        ident_bf = const.tile([P, P], BF16, name="ident_bf")
-        make_identity(nc, ident_bf[:])
 
         w_raw = []
         for o in range(O):
@@ -69,17 +68,17 @@ def tile_biaffine_pa_t_kernel(tc, x1, x2, bw, W_bil, t_ones, lin1, lin2, b_lin, 
         bias_b = const.tile([P, O, 4], BF16, name="bias_b")
 
         load_x(x1, x1_raw, "x1", 0, 1)
+        nc.scalar.dma_start(out=bias_b[:], in_=W_bil[:, D, :].rearrange("o (p c) -> p o c", c=4))
         load_w(0)
+        nc.scalar.dma_start(out=sm_bf[0:16, :], in_=t_ones.rearrange("b x o -> b (x o)"))
+        nc.scalar.dma_start(out=sm_bf[32:48, :], in_=lin1.rearrange("b x o -> b (x o)"))
         load_w(1)
-        nc.sync.dma_start(out=bias_b[:], in_=W_bil[:, D, :].rearrange("o (p c) -> p o c", c=4))
         load_x(x2, x2_raw, "x2", 0, 1)
+        nc.scalar.dma_start(out=bw_b[:], in_=bw.partition_broadcast(P))
         load_x(x1, x1_raw, "x1", 1, 1)
-        nc.sync.dma_start(out=bw_b[:], in_=bw.partition_broadcast(P))
         load_x(x2, x2_raw, "x2", 1, 1)
-        nc.sync.dma_start(out=sm_bf[0:16, :], in_=t_ones.rearrange("b x o -> b (x o)"))
-        nc.sync.dma_start(out=sm_bf[32:48, :], in_=lin1.rearrange("b x o -> b (x o)"))
+        nc.sync.dma_start(out=l2w[:].bitcast(BF16)[0:B, :], in_=lin2.rearrange("b y o -> b (y o)"))
         nc.sync.dma_start(out=bl_b[:], in_=b_lin.partition_broadcast(P))
-        nc.sync.dma_start(out=l2r[0:B, :], in_=lin2.rearrange("b y o -> b (y o)"))
         for b0, nb in LOAD_GROUPS[1:]:
             load_x(x1, x1_raw, "x1", b0, nb)
             load_x(x2, x2_raw, "x2", b0, nb)
@@ -277,34 +276,26 @@ def tile_biaffine_pa_t_kernel(tc, x1, x2, bw, W_bil, t_ones, lin1, lin2, b_lin, 
         def regroup_t(b):
             dst = get_tg(b)[:].rearrange("q (h o r t) -> q h o r t", h=H, o=O, t=4)
             src = tp[b][:].rearrange("q t (h r) -> q h r t", h=H)
-            for h in range(H):
-                nc.gpsimd.tensor_scalar(
-                    out=dst[:, h, 1],
-                    in0=src[:, h],
-                    scalar1=1.0,
-                    scalar2=0.0,
-                    op0=ALU.mult,
-                    op1=ALU.add,
-                )
+            nc.gpsimd.tensor_scalar(
+                out=dst[:, :, 1], in0=src, scalar1=1.0, scalar2=0.0, op0=ALU.mult, op1=ALU.add
+            )
 
         def spread(b):
-            acc = ps_t.tile([P, L, O], F32, name="pt", tag="pt")
-            nc.tensor.matmul(
-                out=acc[:].rearrange("p y o -> p (y o)"),
-                lhsT=ident_bf[:, b : b + 1].to_broadcast([P, P]),
-                rhs=l2r[:],
-                start=True,
-                stop=True,
-            )
+            acc = ps_t.tile([P, 2, P], F32, name="pt", tag="pt")
+            for u in range(2):
+                nc.tensor.transpose(
+                    out=acc[:, u, :], in_=l2t[:, u, b : b + 1].to_broadcast([P, P]), identity=ident[:]
+                )
             sp[b] = acc
 
         def add_x_terms(b):
             stt = keep3.tile([P, H, O, L], F32, name="st")
+            l2_view = sp[b][:].rearrange("p u y -> p (u y)").bitcast(BF16).rearrange("p (y o) -> p y o", o=O)
             for h in range(H):
                 for o in range(O):
                     nc.scalar.activation(
                         out=stt[:, h, o, :],
-                        in_=sp[b][:, :, o],
+                        in_=l2_view[:, :, o],
                         func=ACT.Identity,
                         bias=a_x[:, h, b, o : o + 1],
                         scale=bwn[:, 1:2],
@@ -341,129 +332,136 @@ def tile_biaffine_pa_t_kernel(tc, x1, x2, bw, W_bil, t_ones, lin1, lin2, b_lin, 
         a_l = const.tile([P, H, B, O], F32, name="a_l")
         a_x = const.tile([P, H, B, O], F32, name="a_x")
         bias_f = const.tile([P, O, 4], F32, name="bias_f")
-        sm_s = const.tile([P, H, P], F32, name="sm_s")
+        sm_s = const.tile([P, H, 48], F32, name="sm_s")
 
-        def mix_weights():
+        def mix_weights_1():
             nc.gpsimd.tensor_tensor(out=dif[:], in0=bw_b[:, 1:2], in1=bw_b[:, 0:1], op=ALU.subtract)
+
+        def mix_weights_2():
             nc.scalar.activation(out=bwn[:, 0:1], in_=dif[:], func=ACT.Sigmoid, bias=0.0, scale=-1.0)
             nc.scalar.activation(out=bwn[:, 1:2], in_=dif[:], func=ACT.Sigmoid, bias=0.0, scale=1.0)
 
         def small_pe():
-            sm_t = ps_t.tile([P, H, P], F32, name="pt", tag="pt")
+            sm_t = ps_t.tile([P, 2, H, P], F32, name="pt", tag="pt")
             sm_h = sm[:].rearrange("p (r h) -> p h r", h=H)
             for h in range(H):
-                nc.tensor.transpose(out=sm_t[:, h, :], in_=sm_h[:, h, :], identity=ident[:])
+                nc.tensor.transpose(out=sm_t[:, 0, h, :], in_=sm_h[:, h, :], identity=ident[:])
+            for u in range(2):
+                nc.tensor.transpose(out=sm_t[:, 1, u, :], in_=l2w[:, u * P : (u + 1) * P], identity=ident[:])
             return sm_t
 
         def copy_small(sm_t):
-            nc.scalar.copy(out=sm_s[:], in_=sm_t[:])
+            nc.scalar.copy(out=sm_s[:], in_=sm_t[:, 0, :, 0:48])
+            nc.scalar.copy(out=l2t[:], in_=sm_t[:, 1, :, 0:B])
 
         def x_terms():
             sm_v = sm_s[:].bitcast(BF16).rearrange("p k (row e) -> p k row e", e=2)
-            for h in range(H):
-                nc.gpsimd.tensor_tensor(
-                    out=a_l[:, h],
-                    in0=sm_v[:, h, 32:48, :],
-                    in1=bl_b[:].unsqueeze(1).to_broadcast([P, B, O]),
-                    op=ALU.add,
-                )
-                nc.gpsimd.tensor_scalar(
-                    out=a_x[:, h],
-                    in0=sm_v[:, h, 0:16, :],
-                    scalar1=bwn[:, 0:1],
-                    scalar2=0.0,
-                    op0=ALU.mult,
-                    op1=ALU.add,
-                )
-            al_flat = a_l[:].rearrange("p h b o -> p (h b o)")
-            ax_flat = a_x[:].rearrange("p h b o -> p (h b o)")
-            nc.gpsimd.tensor_scalar(
-                out=al_flat, in0=al_flat, scalar1=bwn[:, 1:2], scalar2=0.0, op0=ALU.mult, op1=ALU.add
+            nc.gpsimd.tensor_tensor(
+                out=a_l[:],
+                in0=sm_v[:, :, 32:48, :],
+                in1=bl_b[:].unsqueeze(1).unsqueeze(1).to_broadcast([P, H, B, O]),
+                op=ALU.add,
             )
-            nc.gpsimd.tensor_tensor(out=ax_flat, in0=ax_flat, in1=al_flat, op=ALU.add)
+            nc.gpsimd.tensor_scalar(
+                out=a_x[:], in0=sm_v[:, :, 0:16, :], scalar1=bwn[:, 0:1], scalar2=0.0, op0=ALU.mult, op1=ALU.add
+            )
+            nc.gpsimd.tensor_scalar(
+                out=a_l[:], in0=a_l[:], scalar1=bwn[:, 1:2], scalar2=0.0, op0=ALU.mult, op1=ALU.add
+            )
+            nc.gpsimd.tensor_tensor(out=a_x[:], in0=a_x[:], in1=a_l[:], op=ALU.add)
 
         transposes(0, 0)
         exit_x(0, 0)
         regroup_w(0, 0, "vector")
-        regroup_w(0, 1, "vector")
-        regroup_w(1, 0, "scalar")
+        regroup_w(0, 1, "scalar")
         quant_x(0, 0)
         quant_w(0, 0)
-        quant_w(0, 1)
         nc.gpsimd.tensor_copy(out=bias_f[:], in_=bias_b[:])
-        mix_weights()
-        transposes(0, 1)
+        regroup_w(1, 0, "vector")
+        quant_w(0, 1)
         stage1(0, 0)
         stage1(0, 1)
-        regroup_w(1, 1, "scalar")
-        t_out(0, 0)
-        sm_t = small_pe()
+        transposes(0, 1)
         transposes(1, 0)
         exit_x(0, 1)
-        copy_small(sm_t)
-        x_terms()
-        t_out(0, 1)
         quant_w(1, 0)
-        quant_w(1, 1)
-        stage1(0, 2)
-        stage1(0, 3)
+        regroup_w(1, 1, "gpsimd")
+        mix_weights_1()
         exit_x(1, 0)
+        t_out(0, 0)
+        t_out(0, 1)
         quant_x(0, 1)
-        t_out(0, 2)
+        quant_w(1, 1)
+        mix_weights_2()
         transposes(1, 1)
         exit_x(1, 1)
-        quant_x(1, 0)
-        t_out(0, 3)
-        quant_x(1, 1)
+        sm_t = small_pe()
+        copy_small(sm_t)
+        x_terms()
+        stage1(0, 2)
+        stage1(0, 3)
         transposes(2, 0)
+        quant_x(1, 0)
+        quant_x(1, 1)
+        t_out(0, 2)
+        t_out(0, 3)
         transposes(2, 1)
 
         for k in range(B):
-            if k > 1:
-                stage2(k - 1, range(H))
             if k > 0:
-                spread(k)
+                stage2(k - 1, range(H))
             if k + 2 < B:
                 exit_x(k + 2, 0)
                 exit_x(k + 2, 1)
-            if k + 1 < B:
+            if k + 1 < B and 1:
                 planar_pe(k + 1, 0)
                 planar_pe(k + 1, 1)
             if k == 0:
-                spread(k)
+                spread(0)
             for h in range(H):
-                if 0 < k < B - 1 or (k == B - 1 and h == 0):
+                if k > 0:
                     t_out(k, h)
                 if k + 1 < B:
                     stage1(k + 1, h)
-                if k == B - 1:
-                    out_exit(k - 1, [h])
-                    quant_t(k, h, 1)
-            if k == 0 or k == B - 2:
+                if k + 1 < B and 0:
+                    planar_pe(k + 1, h)
+            if k < 1 or k == B - 2:
                 planar_exits(k + 1)
                 regroup_t(k + 1)
-            if k == B - 2:
-                t_out_scalar(k + 1, 1)
             add_x_terms(k)
-            if k < B - 2:
-                if k > 0:
-                    out_exit(k - 1, range(H))
+            if k == 0:
+                quant_x(2, 0)
+                quant_x(2, 1)
+                quant_t(0, 0, H)
+            elif k < B - 2:
+                out_exit(k - 1, range(H))
                 quant_t(k, 0, H)
             elif k == B - 2:
                 out_exit(k - 1, [0])
                 quant_t(k, 0, H)
                 out_exit(k - 1, [1])
-            if 0 < k < B - 2:
+            else:
+                quant_t(k, 0, H)
+                for h in range(H):
+                    out_exit(k - 1, [h])
+            if 1 <= k < B - 2:
                 planar_exits(k + 1)
                 regroup_t(k + 1)
-            if k + 2 < B:
+            if 0 < k < B - 2:
                 quant_x(k + 2, 0)
                 quant_x(k + 2, 1)
-            if k == 0:
-                stage2(0, range(H))
-            if k + 3 < B:
+            if k + 3 < B and 2 > 0:
                 transposes(k + 3, 0)
+            if k + 3 < B and 2 > 1:
                 transposes(k + 3, 1)
+            if k < 0:
+                stage2(k, range(H))
+            if k + 3 < B and 2 < 1:
+                transposes(k + 3, 0)
+            if k + 3 < B and 2 < 2:
+                transposes(k + 3, 1)
+            if k + 1 < B:
+                spread(k + 1)
         for h in range(H):
             stage2(B - 1, [h])
             out_exit(B - 1, [h])

@@ -17,7 +17,8 @@ H = L // P
 
 FLOPS = 2 * B * L * D * O * D + 2 * B * O * L * L * D
 
-LOAD_GROUPS = [(1, 1), (2, 1), (3, 1), (4, 2), (6, 2), (8, 2), (10, 2), (12, 2), (14, 2)]
+DIRECT = 2
+LOAD_GROUPS = [(3, 1), (4, 2), (6, 2), (8, 2), (10, 2), (12, 2), (14, 2)]
 
 
 def tile_biaffine_pa_t_kernel(tc, x1, x2, bw, W_bil, t_ones, lin1, lin2, b_lin, out):
@@ -27,7 +28,9 @@ def tile_biaffine_pa_t_kernel(tc, x1, x2, bw, W_bil, t_ones, lin1, lin2, b_lin, 
         stage = ctx.enter_context(tc.tile_pool(name="stage", bufs=2))
         keep3 = ctx.enter_context(tc.tile_pool(name="keep3", bufs=3))
         keep4 = ctx.enter_context(tc.tile_pool(name="keep4", bufs=4))
-        ps_t = ctx.enter_context(tc.psum_pool(name="ps_t", bufs=4))
+        outs = ctx.enter_context(tc.tile_pool(name="outs", bufs=B))
+        ps_t = ctx.enter_context(tc.psum_pool(name="ps_t", bufs=3))
+        ps_s = ctx.enter_context(tc.psum_pool(name="ps_s", bufs=1))
         ps_1 = ctx.enter_context(tc.psum_pool(name="ps_1", bufs=2))
         ps_2 = ctx.enter_context(tc.psum_pool(name="ps_2", bufs=2))
         ctx.enter_context(tc.manual_schedule())
@@ -70,16 +73,18 @@ def tile_biaffine_pa_t_kernel(tc, x1, x2, bw, W_bil, t_ones, lin1, lin2, b_lin, 
         load_x(x1, x1_raw, "x1", 0, 1)
         nc.scalar.dma_start(out=bias_b[:], in_=W_bil[:, D, :].rearrange("o (p c) -> p o c", c=4))
         load_w(0)
+        load_x(x2, x2_raw, "x2", 0, 1)
+        load_w(1)
         nc.scalar.dma_start(out=sm_bf[0:16, :], in_=t_ones.rearrange("b x o -> b (x o)"))
         nc.scalar.dma_start(out=sm_bf[32:48, :], in_=lin1.rearrange("b x o -> b (x o)"))
-        load_w(1)
-        load_x(x2, x2_raw, "x2", 0, 1)
         nc.scalar.dma_start(out=bw_b[:], in_=bw.partition_broadcast(P))
         load_x(x1, x1_raw, "x1", 1, 1)
         load_x(x2, x2_raw, "x2", 1, 1)
+        load_x(x1, x1_raw, "x1", 2, 1)
+        load_x(x2, x2_raw, "x2", 2, 1)
         nc.sync.dma_start(out=l2w[:].bitcast(BF16)[0:B, :], in_=lin2.rearrange("b y o -> b (y o)"))
         nc.sync.dma_start(out=bl_b[:], in_=b_lin.partition_broadcast(P))
-        for b0, nb in LOAD_GROUPS[1:]:
+        for b0, nb in LOAD_GROUPS:
             load_x(x1, x1_raw, "x1", b0, nb)
             load_x(x2, x2_raw, "x2", b0, nb)
 
@@ -138,30 +143,35 @@ def tile_biaffine_pa_t_kernel(tc, x1, x2, bw, W_bil, t_ones, lin1, lin2, b_lin, 
             pt_x[(b, which)] = pt
 
         def exit_x(b, which):
-            g = stage.tile([P, 4 * L], BF16, name="x%dg" % which, align_bytes=64)
+            if b not in xg:
+                g = stage.tile([P, 2 * 4 * L], BF16, name="xg", align_bytes=64)
+                xg[b] = g
+            words = xg[b][:].bitcast(F32)
             if which == 0:
-                dst = g[:].bitcast(F32).rearrange("q (h r u) -> q h r u", h=H, u=2)
-            else:
-                dst = g[:].bitcast(F32).rearrange("q (r h u) -> q h r u", h=H, u=2)
-            if which == 0:
-                nc.scalar.copy(out=dst, in_=pt_x[(b, which)][:].rearrange("q h u r -> q h r u"))
+                nc.scalar.copy(
+                    out=words[:, 0 : 2 * L].rearrange("q (h r u) -> q h r u", h=H, u=2),
+                    in_=pt_x[(b, which)][:].rearrange("q h u r -> q h r u"),
+                )
             else:
                 nc.scalar.copy(
-                    out=g[:].bitcast(F32).rearrange("q (r h u) -> q r h u", h=H, u=2),
+                    out=words[:, 2 * L : 4 * L].rearrange("q (r h u) -> q r h u", h=H, u=2),
                     in_=pt_x[(b, which)][:].rearrange("q h u r -> q r h u"),
                 )
-            xg[(b, which)] = g
 
-        def quant_x(b, which):
-            pool = (keep3, keep4)[which]
-            q = pool.tile([P, L], U32, name="x%dq" % which, align_bytes=64)
-            s = pool.tile([P, L], U8, name="x%ds" % which, align_bytes=64)
-            nc.vector.quantize_mx(out=q[:].bitcast(FP8X4), scales=s[:], in_=xg[(b, which)][:])
-            xq[(b, which)] = (q, s)
+        def quant_x(b, first, last):
+            if b not in xq:
+                q = keep4.tile([P, 2 * L], U32, name="xq", align_bytes=64)
+                s = keep4.tile([P, 2 * L], U8, name="xs", align_bytes=64)
+                xq[b] = (q, s)
+            q, s = xq[b]
+            c0, c1 = first * L, (last + 1) * L
+            nc.vector.quantize_mx(
+                out=q[:, c0:c1].bitcast(FP8X4), scales=s[:, c0:c1], in_=xg[b][:, 4 * c0 : 4 * c1]
+            )
 
         def stage1(b, g):
             o, h = g // H, g % H
-            x1q, x1s = xq[(b, 0)]
+            x1q, x1s = xq[b]
             acc = ps_1.tile([P, 4, P], F32, name="p1", tag="p1")
             for c in range(4):
                 w0 = (o * 4 + c) * P
@@ -205,7 +215,7 @@ def tile_biaffine_pa_t_kernel(tc, x1, x2, bw, W_bil, t_ones, lin1, lin2, b_lin, 
 
         def stage2(b, halves):
             tqt, tst = tq[b]
-            x2q, x2s = xq[(b, 1)]
+            x2q, x2s = xq[b]
             for h in halves:
                 if b == B - 1:
                     acc = ps_t.tile([P, O, L], F32, name="pt", tag="pt")
@@ -217,15 +227,15 @@ def tile_biaffine_pa_t_kernel(tc, x1, x2, bw, W_bil, t_ones, lin1, lin2, b_lin, 
                         out=acc[:, o, :],
                         lhsT=tqt[:, c0 : c0 + P].bitcast(FP8X4),
                         lhsT_scale=tst[:, c0 : c0 + P],
-                        rhs=x2q[:].bitcast(FP8X4),
-                        rhs_scale=x2s[:],
+                        rhs=x2q[:, L : 2 * L].bitcast(FP8X4),
+                        rhs_scale=x2s[:, L : 2 * L],
                         start=True,
                         stop=True,
                     )
                 p2[(b, h)] = acc
 
         def planar_pe(b, cp):
-            x1q, x1s = xq[(b, 0)]
+            x1q, x1s = xq[b]
             acc = ps_t.tile([P, 2, L], F32, name="pt", tag="pt")
             for ci in range(2):
                 w0 = (4 + 2 * cp + ci) * P
@@ -233,8 +243,8 @@ def tile_biaffine_pa_t_kernel(tc, x1, x2, bw, W_bil, t_ones, lin1, lin2, b_lin, 
                     out=acc[:, ci, :],
                     lhsT=w_q[:, w0 : w0 + P].bitcast(FP8X4),
                     lhsT_scale=w_s[:, w0 : w0 + P],
-                    rhs=x1q[:].bitcast(FP8X4),
-                    rhs_scale=x1s[:],
+                    rhs=x1q[:, 0:L].bitcast(FP8X4),
+                    rhs_scale=x1s[:, 0:L],
                     start=True,
                     stop=True,
                 )
@@ -280,31 +290,38 @@ def tile_biaffine_pa_t_kernel(tc, x1, x2, bw, W_bil, t_ones, lin1, lin2, b_lin, 
                 out=dst[:, :, 1], in0=src, scalar1=1.0, scalar2=0.0, op0=ALU.mult, op1=ALU.add
             )
 
-        def spread(b):
-            acc = ps_t.tile([P, 2, P], F32, name="pt", tag="pt")
-            for u in range(2):
-                nc.tensor.transpose(
-                    out=acc[:, u, :], in_=l2t[:, u, b : b + 1].to_broadcast([P, P]), identity=ident[:]
-                )
-            sp[b] = acc
-
-        def add_x_terms(b):
-            stt = keep3.tile([P, H, O, L], F32, name="st")
-            l2_view = sp[b][:].rearrange("p u y -> p (u y)").bitcast(BF16).rearrange("p (y o) -> p y o", o=O)
-            for h in range(H):
-                for o in range(O):
-                    nc.scalar.activation(
-                        out=stt[:, h, o, :],
-                        in_=l2_view[:, :, o],
-                        func=ACT.Identity,
-                        bias=a_x[:, h, b, o : o + 1],
-                        scale=bwn[:, 1:2],
+        def spread(b, nb):
+            acc = ps_s.tile([P, 2, 2, P], F32, name="ps")
+            for i in range(nb):
+                for u in range(2):
+                    nc.tensor.transpose(
+                        out=acc[:, i, u, :],
+                        in_=l2t[:, u, b + i : b + i + 1].to_broadcast([P, P]),
+                        identity=ident[:],
                     )
+                sp[b + i] = acc[:, i]
+
+        def add_x_terms(b, parts):
+            stt = keep3.tile([P, H, O, L], F32, name="st")
+            l2_view = sp[b].rearrange("p u y -> p (u y)").bitcast(BF16).rearrange("p (y o) -> p y o", o=O)
+            for h, o in parts:
+                nc.scalar.activation(
+                    out=stt[:, h, o, :],
+                    in_=l2_view[:, :, o],
+                    func=ACT.Identity,
+                    bias=a_x[:, h, b, o : o + 1],
+                    scale=bwn[:, 1:2],
+                )
             st[b] = stt
+
+        def add_x_difference(b, o):
+            nc.vector.tensor_scalar_add(
+                out=st[b][:, 1, o, :], in0=st[b][:, 0, o, :], scalar1=d_x[:, b, o : o + 1]
+            )
 
         def out_exit(b, halves):
             if b not in ots:
-                ott = keep4.tile([P, H, L, O], F32, name="ot")
+                ott = outs.tile([P, H, L, O], F32, name="ot")
                 ots[b] = ott
             ot = ots[b]
             for h in halves:
@@ -331,6 +348,7 @@ def tile_biaffine_pa_t_kernel(tc, x1, x2, bw, W_bil, t_ones, lin1, lin2, b_lin, 
         bwn = const.tile([P, 2], F32, name="bwn")
         a_l = const.tile([P, H, B, O], F32, name="a_l")
         a_x = const.tile([P, H, B, O], F32, name="a_x")
+        d_x = const.tile([P, B, O], F32, name="d_x")
         bias_f = const.tile([P, O, 4], F32, name="bias_f")
         sm_s = const.tile([P, H, 48], F32, name="sm_s")
 
@@ -342,17 +360,17 @@ def tile_biaffine_pa_t_kernel(tc, x1, x2, bw, W_bil, t_ones, lin1, lin2, b_lin, 
             nc.scalar.activation(out=bwn[:, 1:2], in_=dif[:], func=ACT.Sigmoid, bias=0.0, scale=1.0)
 
         def small_pe():
-            sm_t = ps_t.tile([P, 2, H, P], F32, name="pt", tag="pt")
+            sm_t = ps_t.tile([P, H, P], F32, name="pt", tag="pt")
             sm_h = sm[:].rearrange("p (r h) -> p h r", h=H)
             for h in range(H):
-                nc.tensor.transpose(out=sm_t[:, 0, h, :], in_=sm_h[:, h, :], identity=ident[:])
-            for u in range(2):
-                nc.tensor.transpose(out=sm_t[:, 1, u, :], in_=l2w[:, u * P : (u + 1) * P], identity=ident[:])
-            return sm_t
+                nc.tensor.transpose(out=sm_t[:, h, :], in_=sm_h[:, h, :], identity=ident[:])
+            nc.scalar.copy(out=sm_s[:], in_=sm_t[:, :, 0:48])
 
-        def copy_small(sm_t):
-            nc.scalar.copy(out=sm_s[:], in_=sm_t[:, 0, :, 0:48])
-            nc.scalar.copy(out=l2t[:], in_=sm_t[:, 1, :, 0:B])
+        def lin2_pe():
+            l2p = ps_s.tile([P, 2, P], F32, name="ps")
+            for u in range(2):
+                nc.tensor.transpose(out=l2p[:, u, :], in_=l2w[:, u * P : (u + 1) * P], identity=ident[:])
+            nc.scalar.copy(out=l2t[:], in_=l2p[:, :, 0:B])
 
         def x_terms():
             sm_v = sm_s[:].bitcast(BF16).rearrange("p k (row e) -> p k row e", e=2)
@@ -369,70 +387,69 @@ def tile_biaffine_pa_t_kernel(tc, x1, x2, bw, W_bil, t_ones, lin1, lin2, b_lin, 
                 out=a_l[:], in0=a_l[:], scalar1=bwn[:, 1:2], scalar2=0.0, op0=ALU.mult, op1=ALU.add
             )
             nc.gpsimd.tensor_tensor(out=a_x[:], in0=a_x[:], in1=a_l[:], op=ALU.add)
+            nc.gpsimd.tensor_tensor(out=d_x[:], in0=a_x[:, 1], in1=a_x[:, 0], op=ALU.subtract)
 
         transposes(0, 0)
+        transposes(0, 1)
         exit_x(0, 0)
         regroup_w(0, 0, "vector")
         regroup_w(0, 1, "scalar")
-        quant_x(0, 0)
+        quant_x(0, 0, 0)
         quant_w(0, 0)
         nc.gpsimd.tensor_copy(out=bias_f[:], in_=bias_b[:])
-        regroup_w(1, 0, "vector")
+        mix_weights_1()
+        exit_x(0, 1)
         quant_w(0, 1)
         stage1(0, 0)
         stage1(0, 1)
-        transposes(0, 1)
+        regroup_w(1, 0, "vector")
+        regroup_w(1, 1, "scalar")
+        quant_x(0, 1, 1)
         transposes(1, 0)
-        exit_x(0, 1)
-        quant_w(1, 0)
-        regroup_w(1, 1, "gpsimd")
-        mix_weights_1()
-        exit_x(1, 0)
+        transposes(1, 1)
         t_out(0, 0)
         t_out(0, 1)
-        quant_x(0, 1)
-        quant_w(1, 1)
+        exit_x(1, 0)
         mix_weights_2()
-        transposes(1, 1)
+        quant_w(1, 0)
+        quant_w(1, 1)
         exit_x(1, 1)
-        sm_t = small_pe()
-        copy_small(sm_t)
+        small_pe()
         x_terms()
         stage1(0, 2)
         stage1(0, 3)
+        quant_x(1, 0, 1)
+        lin2_pe()
         transposes(2, 0)
-        quant_x(1, 0)
-        quant_x(1, 1)
         t_out(0, 2)
         t_out(0, 3)
         transposes(2, 1)
+        spread(0, 1)
 
         for k in range(B):
-            if k > 0:
+            groups = range(O * H) if k < DIRECT else range(H)
+            if k > 1:
                 stage2(k - 1, range(H))
+            parts = [(0, 0), (0, 1), (1, 0), (1, 1)]
             if k + 2 < B:
                 exit_x(k + 2, 0)
                 exit_x(k + 2, 1)
-            if k + 1 < B and 1:
-                planar_pe(k + 1, 0)
-                planar_pe(k + 1, 1)
+            add_x_terms(k, parts)
+            if k + 1 < DIRECT:
+                for g in range(O * H):
+                    if k > 0:
+                        t_out(k, g)
+                    stage1(k + 1, g)
+            else:
+                for g in groups:
+                    if k > 0:
+                        t_out(k, g)
+                    if k + 1 < B and g < H:
+                        planar_pe(k + 1, g)
+                        stage1(k + 1, g)
             if k == 0:
-                spread(0)
-            for h in range(H):
-                if k > 0:
-                    t_out(k, h)
-                if k + 1 < B:
-                    stage1(k + 1, h)
-                if k + 1 < B and 0:
-                    planar_pe(k + 1, h)
-            if k < 1 or k == B - 2:
-                planar_exits(k + 1)
-                regroup_t(k + 1)
-            add_x_terms(k)
-            if k == 0:
-                quant_x(2, 0)
-                quant_x(2, 1)
                 quant_t(0, 0, H)
+                quant_x(2, 0, 1)
             elif k < B - 2:
                 out_exit(k - 1, range(H))
                 quant_t(k, 0, H)
@@ -442,26 +459,20 @@ def tile_biaffine_pa_t_kernel(tc, x1, x2, bw, W_bil, t_ones, lin1, lin2, b_lin, 
                 out_exit(k - 1, [1])
             else:
                 quant_t(k, 0, H)
-                for h in range(H):
-                    out_exit(k - 1, [h])
-            if 1 <= k < B - 2:
+                out_exit(k - 1, range(H))
+            if DIRECT <= k + 1 < B:
                 planar_exits(k + 1)
                 regroup_t(k + 1)
             if 0 < k < B - 2:
-                quant_x(k + 2, 0)
-                quant_x(k + 2, 1)
-            if k + 3 < B and 2 > 0:
-                transposes(k + 3, 0)
-            if k + 3 < B and 2 > 1:
-                transposes(k + 3, 1)
-            if k < 0:
+                quant_x(k + 2, 0, 1)
+            if k < 1:
                 stage2(k, range(H))
-            if k + 3 < B and 2 < 1:
+            if k == 0:
+                spread(1, 1)
+            if k + 3 < B:
                 transposes(k + 3, 0)
-            if k + 3 < B and 2 < 2:
                 transposes(k + 3, 1)
-            if k + 1 < B:
-                spread(k + 1)
-        for h in range(H):
-            stage2(B - 1, [h])
-            out_exit(B - 1, [h])
+            if k % 2 == 1 and k + 1 < B:
+                spread(k + 1, 2)
+        stage2(B - 1, range(H))
+        out_exit(B - 1, range(H))

@@ -17,7 +17,7 @@ H = L // P
 
 FLOPS = 2 * B * L * D * O * D + 2 * B * O * L * L * D
 
-DIRECT = 2
+DIRECT = 1
 LOAD_GROUPS = [(3, 1), (4, 2), (6, 2), (8, 2), (10, 2), (12, 2), (14, 2)]
 
 
@@ -29,22 +29,24 @@ def tile_biaffine_pa_t_kernel(tc, x1, x2, bw, W_bil, t_ones, lin1, lin2, b_lin, 
         keep3 = ctx.enter_context(tc.tile_pool(name="keep3", bufs=3))
         keep4 = ctx.enter_context(tc.tile_pool(name="keep4", bufs=4))
         outs = ctx.enter_context(tc.tile_pool(name="outs", bufs=B))
-        ps_t = ctx.enter_context(tc.psum_pool(name="ps_t", bufs=3))
-        ps_s = ctx.enter_context(tc.psum_pool(name="ps_s", bufs=1))
+        ps_t = ctx.enter_context(tc.psum_pool(name="ps_t", bufs=4))
         ps_1 = ctx.enter_context(tc.psum_pool(name="ps_1", bufs=2))
         ps_2 = ctx.enter_context(tc.psum_pool(name="ps_2", bufs=2))
         ctx.enter_context(tc.manual_schedule())
 
+        wz = const.tile([P, 512], BF16, name="wz")
+        nc.vector.memset(wz[:], 0.0)
         warm = const.tile([P, 1], F32, name="warm")
         nc.vector.memset(warm[:], 0.0)
         warm_o = const.tile([P, 1], F32, name="warm_o")
         sm = const.tile([P, 256], F32, name="sm")
         nc.vector.memset(sm[:], 0.0)
-        l2w = const.tile([P, L], F32, name="l2w")
-        nc.vector.memset(l2w[:], 0.0)
-        l2t = const.tile([P, 2, B], F32, name="l2t")
+        l2r = const.tile([P, L * O], BF16, name="l2r")
+        nc.vector.memset(l2r[:], 0.0)
         ident = const.tile([P, P], F32, name="ident")
         make_identity(nc, ident[:])
+        ident_bf = const.tile([P, P], BF16, name="ident_bf")
+        nc.vector.tensor_copy(out=ident_bf[:], in_=ident[:])
 
         w_raw = []
         for o in range(O):
@@ -82,7 +84,7 @@ def tile_biaffine_pa_t_kernel(tc, x1, x2, bw, W_bil, t_ones, lin1, lin2, b_lin, 
         load_x(x2, x2_raw, "x2", 1, 1)
         load_x(x1, x1_raw, "x1", 2, 1)
         load_x(x2, x2_raw, "x2", 2, 1)
-        nc.sync.dma_start(out=l2w[:].bitcast(BF16)[0:B, :], in_=lin2.rearrange("b y o -> b (y o)"))
+        nc.sync.dma_start(out=l2r[0:B, :], in_=lin2.rearrange("b y o -> b (y o)"))
         nc.sync.dma_start(out=bl_b[:], in_=b_lin.partition_broadcast(P))
         for b0, nb in LOAD_GROUPS:
             load_x(x1, x1_raw, "x1", b0, nb)
@@ -290,24 +292,34 @@ def tile_biaffine_pa_t_kernel(tc, x1, x2, bw, W_bil, t_ones, lin1, lin2, b_lin, 
                 out=dst[:, :, 1], in0=src, scalar1=1.0, scalar2=0.0, op0=ALU.mult, op1=ALU.add
             )
 
-        def spread(b, nb):
-            acc = ps_s.tile([P, 2, 2, P], F32, name="ps")
-            for i in range(nb):
-                for u in range(2):
-                    nc.tensor.transpose(
-                        out=acc[:, i, u, :],
-                        in_=l2t[:, u, b + i : b + i + 1].to_broadcast([P, P]),
-                        identity=ident[:],
-                    )
-                sp[b + i] = acc[:, i]
+        def spread(b):
+            acc = ps_t.tile([P, L, O], F32, name="pt", tag="pt")
+            nc.tensor.matmul(
+                out=acc[:].rearrange("p y o -> p (y o)"),
+                lhsT=ident_bf[:, b : b + 1].to_broadcast([P, P]),
+                rhs=l2r[:],
+                start=True,
+                stop=True,
+            )
+            sp[b] = acc
+
+        def warm_up(n):
+            acc = ps_2.tile([P, O, L], F32, name="p2", tag="p2")
+            for i in range(n):
+                nc.tensor.matmul(
+                    out=acc[:].rearrange("p o y -> p (o y)"),
+                    lhsT=wz[:, 0:P],
+                    rhs=wz[:],
+                    start=True,
+                    stop=True,
+                )
 
         def add_x_terms(b, parts):
             stt = keep3.tile([P, H, O, L], F32, name="st")
-            l2_view = sp[b].rearrange("p u y -> p (u y)").bitcast(BF16).rearrange("p (y o) -> p y o", o=O)
             for h, o in parts:
                 nc.scalar.activation(
                     out=stt[:, h, o, :],
-                    in_=l2_view[:, :, o],
+                    in_=sp[b][:, :, o],
                     func=ACT.Identity,
                     bias=a_x[:, h, b, o : o + 1],
                     scale=bwn[:, 1:2],
@@ -366,12 +378,6 @@ def tile_biaffine_pa_t_kernel(tc, x1, x2, bw, W_bil, t_ones, lin1, lin2, b_lin, 
                 nc.tensor.transpose(out=sm_t[:, h, :], in_=sm_h[:, h, :], identity=ident[:])
             nc.scalar.copy(out=sm_s[:], in_=sm_t[:, :, 0:48])
 
-        def lin2_pe():
-            l2p = ps_s.tile([P, 2, P], F32, name="ps")
-            for u in range(2):
-                nc.tensor.transpose(out=l2p[:, u, :], in_=l2w[:, u * P : (u + 1) * P], identity=ident[:])
-            nc.scalar.copy(out=l2t[:], in_=l2p[:, :, 0:B])
-
         def x_terms():
             sm_v = sm_s[:].bitcast(BF16).rearrange("p k (row e) -> p k row e", e=2)
             nc.gpsimd.tensor_tensor(
@@ -389,8 +395,10 @@ def tile_biaffine_pa_t_kernel(tc, x1, x2, bw, W_bil, t_ones, lin1, lin2, b_lin, 
             nc.gpsimd.tensor_tensor(out=a_x[:], in0=a_x[:], in1=a_l[:], op=ALU.add)
             nc.gpsimd.tensor_tensor(out=d_x[:], in0=a_x[:, 1], in1=a_x[:, 0], op=ALU.subtract)
 
+        warm_up(4)
         transposes(0, 0)
         transposes(0, 1)
+        warm_up(2)
         exit_x(0, 0)
         regroup_w(0, 0, "vector")
         regroup_w(0, 1, "scalar")
@@ -407,6 +415,7 @@ def tile_biaffine_pa_t_kernel(tc, x1, x2, bw, W_bil, t_ones, lin1, lin2, b_lin, 
         quant_x(0, 1, 1)
         transposes(1, 0)
         transposes(1, 1)
+        warm_up(2)
         t_out(0, 0)
         t_out(0, 1)
         exit_x(1, 0)
@@ -419,34 +428,33 @@ def tile_biaffine_pa_t_kernel(tc, x1, x2, bw, W_bil, t_ones, lin1, lin2, b_lin, 
         stage1(0, 2)
         stage1(0, 3)
         quant_x(1, 0, 1)
-        lin2_pe()
         transposes(2, 0)
         t_out(0, 2)
         t_out(0, 3)
         transposes(2, 1)
-        spread(0, 1)
 
         for k in range(B):
             groups = range(O * H) if k < DIRECT else range(H)
-            if k > 1:
+            if k > 0:
                 stage2(k - 1, range(H))
-            parts = [(0, 0), (0, 1), (1, 0), (1, 1)]
             if k + 2 < B:
                 exit_x(k + 2, 0)
                 exit_x(k + 2, 1)
-            add_x_terms(k, parts)
-            if k + 1 < DIRECT:
-                for g in range(O * H):
-                    if k > 0:
-                        t_out(k, g)
-                    stage1(k + 1, g)
-            else:
-                for g in groups:
-                    if k > 0:
-                        t_out(k, g)
-                    if k + 1 < B and g < H:
-                        planar_pe(k + 1, g)
-                        stage1(k + 1, g)
+            for g in groups:
+                if k > 0:
+                    t_out(k, g)
+                if 0 < k < DIRECT and g < H:
+                    stage1(k, g + H)
+                if k + 1 < B and g >= len(groups) - H:
+                    if k + 1 >= DIRECT:
+                        planar_pe(k + 1, g - len(groups) + H)
+                    stage1(k + 1, g - len(groups) + H)
+            if k == 0:
+                spread(0)
+            if DIRECT <= k + 1 < B and k < 1:
+                planar_exits(k + 1)
+                regroup_t(k + 1)
+            add_x_terms(k, [(0, 0), (0, 1), (1, 0), (1, 1)])
             if k == 0:
                 quant_t(0, 0, H)
                 quant_x(2, 0, 1)
@@ -460,19 +468,18 @@ def tile_biaffine_pa_t_kernel(tc, x1, x2, bw, W_bil, t_ones, lin1, lin2, b_lin, 
             else:
                 quant_t(k, 0, H)
                 out_exit(k - 1, range(H))
-            if DIRECT <= k + 1 < B:
+            if DIRECT <= k + 1 < B and k >= 1:
                 planar_exits(k + 1)
                 regroup_t(k + 1)
             if 0 < k < B - 2:
                 quant_x(k + 2, 0, 1)
-            if k < 1:
+            if k < 0:
                 stage2(k, range(H))
-            if k == 0:
-                spread(1, 1)
             if k + 3 < B:
                 transposes(k + 3, 0)
+            if k + 3 < B:
                 transposes(k + 3, 1)
-            if k % 2 == 1 and k + 1 < B:
-                spread(k + 1, 2)
+            if k + 1 < B:
+                spread(k + 1)
         stage2(B - 1, range(H))
         out_exit(B - 1, range(H))

@@ -337,19 +337,21 @@ def tile_biaffine_pa_t_kernel(tc, x1, x2, bw, W_bil, t_ones, lin1, lin2, b_lin, 
                 ots[b] = ott
             ot = ots[b]
             for h in halves:
-                nc.vector.scalar_tensor_tensor(
-                    out=ot[:, h],
-                    in0=p2[(b, h)][:].rearrange("p o y -> p y o"),
-                    scalar=bwn[:, 0:1],
-                    in1=st[b][:, h].rearrange("p o y -> p y o"),
-                    op0=ALU.mult,
-                    op1=ALU.add,
-                )
-                if b >= B - 3:
-                    nc.sync.dma_start(
-                        out=out[b].rearrange("(p h) y o -> p h (y o)", h=H)[:, h, :],
-                        in_=ot[:, h].rearrange("p y o -> p (y o)"),
+                cuts = [0, L // 2, L] if b == B - 1 and h == H - 1 else [0, L]
+                for y0, y1 in zip(cuts, cuts[1:]):
+                    nc.vector.scalar_tensor_tensor(
+                        out=ot[:, h, y0:y1],
+                        in0=p2[(b, h)][:, :, y0:y1].rearrange("p o y -> p y o"),
+                        scalar=bwn[:, 0:1],
+                        in1=st[b][:, h, :, y0:y1].rearrange("p o y -> p y o"),
+                        op0=ALU.mult,
+                        op1=ALU.add,
                     )
+                    if b >= B - 3:
+                        nc.sync.dma_start(
+                            out=out[b].rearrange("(p h) y o -> p h y o", h=H)[:, h, y0:y1],
+                            in_=ot[:, h, y0:y1],
+                        )
             if b < B - 3:
                 nc.sync.dma_start(
                     out=out[b].rearrange("(p h) y o -> p (h y o)", h=H),
@@ -395,8 +397,9 @@ def tile_biaffine_pa_t_kernel(tc, x1, x2, bw, W_bil, t_ones, lin1, lin2, b_lin, 
             nc.gpsimd.tensor_tensor(out=a_x[:], in0=a_x[:], in1=a_l[:], op=ALU.add)
             nc.gpsimd.tensor_tensor(out=d_x[:], in0=a_x[:, 1], in1=a_x[:, 0], op=ALU.subtract)
 
-        warm_up(4)
+        warm_up(5)
         transposes(0, 0)
+        warm_up(2)
         transposes(0, 1)
         warm_up(2)
         exit_x(0, 0)

from contextlib import ExitStack

import concourse.mybir as mybir
from concourse.masks import make_identity

F32 = mybir.dt.float32
BF16 = mybir.dt.bfloat16
U32 = mybir.dt.uint32
U8 = mybir.dt.uint8
FP8X4 = mybir.dt.float8_e4m3fn_x4
ACT = mybir.ActivationFunctionType
ALU = mybir.AluOpType

P = 128
B, L, D, O = 16, 256, 512, 2
H = L // P

FLOPS = 2 * B * L * D * O * D + 2 * B * O * L * L * D

DIRECT = 1
LOAD_GROUPS = [(3, 1), (4, 2), (6, 2), (8, 2), (10, 2), (12, 2), (14, 2)]


def tile_biaffine_pa_t_kernel(tc, x1, x2, bw, W_bil, t_ones, lin1, lin2, b_lin, out):
    nc = tc.nc
    with ExitStack() as ctx:
        const = ctx.enter_context(tc.tile_pool(name="const", bufs=1))
        stage = ctx.enter_context(tc.tile_pool(name="stage", bufs=2))
        keep3 = ctx.enter_context(tc.tile_pool(name="keep3", bufs=3))
        keep4 = ctx.enter_context(tc.tile_pool(name="keep4", bufs=4))
        outs = ctx.enter_context(tc.tile_pool(name="outs", bufs=B))
        ps_t = ctx.enter_context(tc.psum_pool(name="ps_t", bufs=4))
        ps_1 = ctx.enter_context(tc.psum_pool(name="ps_1", bufs=2))
        ps_2 = ctx.enter_context(tc.psum_pool(name="ps_2", bufs=2))
        ctx.enter_context(tc.manual_schedule())

        wz = const.tile([P, 512], BF16, name="wz")
        nc.vector.memset(wz[:], 0.0)
        warm = const.tile([P, 1], F32, name="warm")
        nc.vector.memset(warm[:], 0.0)
        warm_o = const.tile([P, 1], F32, name="warm_o")
        sm = const.tile([P, 256], F32, name="sm")
        nc.vector.memset(sm[:], 0.0)
        l2r = const.tile([P, L * O], BF16, name="l2r")
        nc.vector.memset(l2r[:], 0.0)
        ident = const.tile([P, P], F32, name="ident")
        make_identity(nc, ident[:])
        ident_bf = const.tile([P, P], BF16, name="ident_bf")
        nc.vector.tensor_copy(out=ident_bf[:], in_=ident[:])

        w_raw = []
        for o in range(O):
            wr = const.tile([P, 4, D], BF16, name="w_raw%d" % o)
            w_raw.append(wr)
        x1_raw = {}
        x2_raw = {}

        def load_w(o):
            nc.sync.dma_start(
                out=w_raw[o][:].rearrange("q t j -> q (t j)"),
                in_=W_bil[o, 0:D, :].rearrange("(q t) j -> q (t j)", t=4),
            )

        def load_x(src, store, label, b0, nb):
            xr = const.tile([P, nb, H * D], BF16, name="%s_raw%d" % (label, b0))
            nc.sync.dma_start(out=xr[:], in_=src[b0 : b0 + nb].rearrange("b (p h) i -> p b (h i)", h=H))
            for k in range(nb):
                store[b0 + k] = (xr, k)

        sm_bf = sm[:].bitcast(BF16)
        bw_b = const.tile([P, 2], BF16, name="bw_b")
        bl_b = const.tile([P, 2], BF16, name="bl_b")
        bias_b = const.tile([P, O, 4], BF16, name="bias_b")

        load_x(x1, x1_raw, "x1", 0, 1)
        nc.scalar.dma_start(out=bias_b[:], in_=W_bil[:, D, :].rearrange("o (p c) -> p o c", c=4))
        load_w(0)
        load_x(x2, x2_raw, "x2", 0, 1)
        load_w(1)
        nc.scalar.dma_start(out=sm_bf[0:16, :], in_=t_ones.rearrange("b x o -> b (x o)"))
        nc.scalar.dma_start(out=sm_bf[32:48, :], in_=lin1.rearrange("b x o -> b (x o)"))
        nc.scalar.dma_start(out=bw_b[:], in_=bw.partition_broadcast(P))
        load_x(x1, x1_raw, "x1", 1, 1)
        load_x(x2, x2_raw, "x2", 1, 1)
        load_x(x1, x1_raw, "x1", 2, 1)
        load_x(x2, x2_raw, "x2", 2, 1)
        nc.sync.dma_start(out=l2r[0:B, :], in_=lin2.rearrange("b y o -> b (y o)"))
        nc.sync.dma_start(out=bl_b[:], in_=b_lin.partition_broadcast(P))
        for b0, nb in LOAD_GROUPS:
            load_x(x1, x1_raw, "x1", b0, nb)
            load_x(x2, x2_raw, "x2", b0, nb)

        nc.scalar.activation(out=warm_o[:], in_=warm[:], func=ACT.Sigmoid, bias=0.0, scale=1.0)

        w_q = const.tile([P, O * D], U32, name="w_q", align_bytes=64)
        w_s = const.tile([P, O * D], U8, name="w_s", align_bytes=64)
        w_g = []
        for o in range(O):
            wg = const.tile([P, 4 * D], BF16, name="w_g%d" % o, align_bytes=64)
            w_g.append(wg)

        def regroup_w(o, uj, engine):
            dst = w_g[o][:].rearrange("q (uj ej m t) -> q uj ej m t", uj=2, ej=2, t=4)
            src = w_raw[o][:].rearrange("q t (m uj ej) -> q uj ej m t", uj=2, ej=2)
            if engine == "vector":
                nc.vector.tensor_copy(out=dst[:, uj], in_=src[:, uj])
            elif engine == "scalar":
                nc.scalar.copy(out=dst[:, uj], in_=src[:, uj])
            else:
                nc.gpsimd.tensor_scalar(
                    out=dst[:, uj], in0=src[:, uj], scalar1=1.0, scalar2=0.0, op0=ALU.mult, op1=ALU.add
                )

        def quant_w(o, uj):
            c0 = o * D + uj * 256
            nc.vector.quantize_mx(
                out=w_q[:, c0 : c0 + 256].bitcast(FP8X4),
                scales=w_s[:, c0 : c0 + 256],
                in_=w_g[o][:, uj * 1024 : uj * 1024 + 1024],
            )

        pt_x = {}
        xg = {}
        xq = {}
        p1 = {}
        tg = {}
        tq = {}
        p2 = {}
        pp = {}
        tp = {}
        st = {}
        sp = {}
        ots = {}

        def transposes(b, which):
            xr, k = (x1_raw, x2_raw)[which][b]
            words = xr[:].bitcast(F32)
            pt = ps_t.tile([P, H, 2, P], F32, name="pt", tag="pt")
            for h in range(H):
                for u in range(2):
                    c0 = h * 256
                    nc.tensor.transpose(
                        out=pt[:, h, u, :], in_=words[:, k, c0 + u : c0 + 256 : 2], identity=ident[:]
                    )
            pt_x[(b, which)] = pt

        def exit_x(b, which):
            if b not in xg:
                g = stage.tile([P, 2 * 4 * L], BF16, name="xg", align_bytes=64)
                xg[b] = g
            words = xg[b][:].bitcast(F32)
            if which == 0:
                nc.scalar.copy(
                    out=words[:, 0 : 2 * L].rearrange("q (h r u) -> q h r u", h=H, u=2),
                    in_=pt_x[(b, which)][:].rearrange("q h u r -> q h r u"),
                )
            else:
                nc.scalar.copy(
                    out=words[:, 2 * L : 4 * L].rearrange("q (r h u) -> q r h u", h=H, u=2),
                    in_=pt_x[(b, which)][:].rearrange("q h u r -> q r h u"),
                )

        def quant_x(b, first, last):
            if b not in xq:
                q = keep4.tile([P, 2 * L], U32, name="xq", align_bytes=64)
                s = keep4.tile([P, 2 * L], U8, name="xs", align_bytes=64)
                xq[b] = (q, s)
            q, s = xq[b]
            c0, c1 = first * L, (last + 1) * L
            nc.vector.quantize_mx(
                out=q[:, c0:c1].bitcast(FP8X4), scales=s[:, c0:c1], in_=xg[b][:, 4 * c0 : 4 * c1]
            )

        def stage1(b, g):
            o, h = g // H, g % H
            x1q, x1s = xq[b]
            acc = ps_1.tile([P, 4, P], F32, name="p1", tag="p1")
            for c in range(4):
                w0 = (o * 4 + c) * P
                nc.tensor.matmul_mx(
                    out=acc[:, c, :],
                    lhsT=w_q[:, w0 : w0 + P].bitcast(FP8X4),
                    lhsT_scale=w_s[:, w0 : w0 + P],
                    rhs=x1q[:, h * P : (h + 1) * P].bitcast(FP8X4),
                    rhs_scale=x1s[:, h * P : (h + 1) * P],
                    start=True,
                    stop=True,
                )
            p1[(b, g)] = acc

        def get_tg(b):
            if b not in tg:
                tgt = stage.tile([P, 4 * O * L], BF16, name="tg", align_bytes=64)
                tg[b] = tgt
            return tg[b]

        def t_out(b, g):
            o, h = g // H, g % H
            view = get_tg(b)[:].rearrange("q (h o r c) -> q h o r c", h=H, o=O, c=4)
            nc.vector.tensor_tensor(
                out=view[:, h, o],
                in0=p1[(b, g)][:].rearrange("q c r -> q r c"),
                in1=bias_f[:, o, :].unsqueeze(1).to_broadcast([P, P, 4]),
                op=ALU.add,
            )

        def quant_t(b, h0, nh):
            if b not in tq:
                tqt = stage.tile([P, O * L], U32, name="tq", align_bytes=64)
                tst = stage.tile([P, O * L], U8, name="ts", align_bytes=64)
                tq[b] = (tqt, tst)
            tqt, tst = tq[b]
            c0, c1 = h0 * L, (h0 + nh) * L
            nc.vector.quantize_mx(
                out=tqt[:, c0:c1].bitcast(FP8X4), scales=tst[:, c0:c1], in_=tg[b][:, 4 * c0 : 4 * c1]
            )

        def stage2(b, halves):
            tqt, tst = tq[b]
            x2q, x2s = xq[b]
            for h in halves:
                if b == B - 1:
                    acc = ps_t.tile([P, O, L], F32, name="pt", tag="pt")
                else:
                    acc = ps_2.tile([P, O, L], F32, name="p2", tag="p2")
                for o in range(O):
                    c0 = (h * O + o) * P
                    nc.tensor.matmul_mx(
                        out=acc[:, o, :],
                        lhsT=tqt[:, c0 : c0 + P].bitcast(FP8X4),
                        lhsT_scale=tst[:, c0 : c0 + P],
                        rhs=x2q[:, L : 2 * L].bitcast(FP8X4),
                        rhs_scale=x2s[:, L : 2 * L],
                        start=True,
                        stop=True,
                    )
                p2[(b, h)] = acc

        def planar_pe(b, cp):
            x1q, x1s = xq[b]
            acc = ps_t.tile([P, 2, L], F32, name="pt", tag="pt")
            for ci in range(2):
                w0 = (4 + 2 * cp + ci) * P
                nc.tensor.matmul_mx(
                    out=acc[:, ci, :],
                    lhsT=w_q[:, w0 : w0 + P].bitcast(FP8X4),
                    lhsT_scale=w_s[:, w0 : w0 + P],
                    rhs=x1q[:, 0:L].bitcast(FP8X4),
                    rhs_scale=x1s[:, 0:L],
                    start=True,
                    stop=True,
                )
            pp[(b, cp)] = acc

        def planar_exits(b):
            tpt = stage.tile([P, 4, L], BF16, name="tp")
            for c in range(4):
                nc.scalar.activation(
                    out=tpt[:, c, :],
                    in_=pp[(b, c // 2)][:, c % 2, :],
                    func=ACT.Identity,
                    bias=bias_f[:, 1, c : c + 1],
                    scale=1.0,
                )
            tp[b] = tpt

        def t_out_scalar(b, g):
            tpt = stage.tile([P, 4, P], BF16, name="tp1")
            for c in range(4):
                nc.scalar.activation(
                    out=tpt[:, c, :],
                    in_=p1[(b, g)][:, c, :],
                    func=ACT.Identity,
                    bias=bias_f[:, g // H, c : c + 1],
                    scale=1.0,
                )
            o, h = g // H, g % H
            dst = get_tg(b)[:].rearrange("q (h o r t) -> q h o r t", h=H, o=O, t=4)
            nc.gpsimd.tensor_scalar(
                out=dst[:, h, o],
                in0=tpt[:].rearrange("q t r -> q r t"),
                scalar1=1.0,
                scalar2=0.0,
                op0=ALU.mult,
                op1=ALU.add,
            )

        def regroup_t(b):
            dst = get_tg(b)[:].rearrange("q (h o r t) -> q h o r t", h=H, o=O, t=4)
            src = tp[b][:].rearrange("q t (h r) -> q h r t", h=H)
            nc.gpsimd.tensor_scalar(
                out=dst[:, :, 1], in0=src, scalar1=1.0, scalar2=0.0, op0=ALU.mult, op1=ALU.add
            )

        def spread(b):
            acc = ps_t.tile([P, L, O], F32, name="pt", tag="pt")
            nc.tensor.matmul(
                out=acc[:].rearrange("p y o -> p (y o)"),
                lhsT=ident_bf[:, b : b + 1].to_broadcast([P, P]),
                rhs=l2r[:],
                start=True,
                stop=True,
            )
            sp[b] = acc

        def warm_up(n):
            acc = ps_2.tile([P, O, L], F32, name="p2", tag="p2")
            for i in range(n):
                nc.tensor.matmul(
                    out=acc[:].rearrange("p o y -> p (o y)"),
                    lhsT=wz[:, 0:P],
                    rhs=wz[:],
                    start=True,
                    stop=True,
                )

        def add_x_terms(b, parts):
            stt = keep3.tile([P, H, O, L], F32, name="st")
            for h, o in parts:
                nc.scalar.activation(
                    out=stt[:, h, o, :],
                    in_=sp[b][:, :, o],
                    func=ACT.Identity,
                    bias=a_x[:, h, b, o : o + 1],
                    scale=bwn[:, 1:2],
                )
            st[b] = stt

        def add_x_difference(b, o):
            nc.vector.tensor_scalar_add(
                out=st[b][:, 1, o, :], in0=st[b][:, 0, o, :], scalar1=d_x[:, b, o : o + 1]
            )

        def out_exit(b, halves):
            if b not in ots:
                ott = outs.tile([P, H, L, O], F32, name="ot")
                ots[b] = ott
            ot = ots[b]
            for h in halves:
                cuts = [0, L // 2, L] if b == B - 1 and h == H - 1 else [0, L]
                for y0, y1 in zip(cuts, cuts[1:]):
                    nc.vector.scalar_tensor_tensor(
                        out=ot[:, h, y0:y1],
                        in0=p2[(b, h)][:, :, y0:y1].rearrange("p o y -> p y o"),
                        scalar=bwn[:, 0:1],
                        in1=st[b][:, h, :, y0:y1].rearrange("p o y -> p y o"),
                        op0=ALU.mult,
                        op1=ALU.add,
                    )
                    if b >= B - 3:
                        nc.sync.dma_start(
                            out=out[b].rearrange("(p h) y o -> p h y o", h=H)[:, h, y0:y1],
                            in_=ot[:, h, y0:y1],
                        )
            if b < B - 3:
                nc.sync.dma_start(
                    out=out[b].rearrange("(p h) y o -> p (h y o)", h=H),
                    in_=ot[:].rearrange("p h y o -> p (h y o)"),
                )

        dif = const.tile([P, 1], F32, name="dif")
        bwn = const.tile([P, 2], F32, name="bwn")
        a_l = const.tile([P, H, B, O], F32, name="a_l")
        a_x = const.tile([P, H, B, O], F32, name="a_x")
        d_x = const.tile([P, B, O], F32, name="d_x")
        bias_f = const.tile([P, O, 4], F32, name="bias_f")
        sm_s = const.tile([P, H, 48], F32, name="sm_s")

        def mix_weights_1():
            nc.gpsimd.tensor_tensor(out=dif[:], in0=bw_b[:, 1:2], in1=bw_b[:, 0:1], op=ALU.subtract)

        def mix_weights_2():
            nc.scalar.activation(out=bwn[:, 0:1], in_=dif[:], func=ACT.Sigmoid, bias=0.0, scale=-1.0)
            nc.scalar.activation(out=bwn[:, 1:2], in_=dif[:], func=ACT.Sigmoid, bias=0.0, scale=1.0)

        def small_pe():
            sm_t = ps_t.tile([P, H, P], F32, name="pt", tag="pt")
            sm_h = sm[:].rearrange("p (r h) -> p h r", h=H)
            for h in range(H):
                nc.tensor.transpose(out=sm_t[:, h, :], in_=sm_h[:, h, :], identity=ident[:])
            nc.scalar.copy(out=sm_s[:], in_=sm_t[:, :, 0:48])

        def x_terms():
            sm_v = sm_s[:].bitcast(BF16).rearrange("p k (row e) -> p k row e", e=2)
            nc.gpsimd.tensor_tensor(
                out=a_l[:],
                in0=sm_v[:, :, 32:48, :],
                in1=bl_b[:].unsqueeze(1).unsqueeze(1).to_broadcast([P, H, B, O]),
                op=ALU.add,
            )
            nc.gpsimd.tensor_scalar(
                out=a_x[:], in0=sm_v[:, :, 0:16, :], scalar1=bwn[:, 0:1], scalar2=0.0, op0=ALU.mult, op1=ALU.add
            )
            nc.gpsimd.tensor_scalar(
                out=a_l[:], in0=a_l[:], scalar1=bwn[:, 1:2], scalar2=0.0, op0=ALU.mult, op1=ALU.add
            )
            nc.gpsimd.tensor_tensor(out=a_x[:], in0=a_x[:], in1=a_l[:], op=ALU.add)
            nc.gpsimd.tensor_tensor(out=d_x[:], in0=a_x[:, 1], in1=a_x[:, 0], op=ALU.subtract)

        warm_up(5)
        transposes(0, 0)
        warm_up(2)
        transposes(0, 1)
        warm_up(2)
        exit_x(0, 0)
        regroup_w(0, 0, "vector")
        regroup_w(0, 1, "scalar")
        quant_x(0, 0, 0)
        quant_w(0, 0)
        nc.gpsimd.tensor_copy(out=bias_f[:], in_=bias_b[:])
        mix_weights_1()
        exit_x(0, 1)
        quant_w(0, 1)
        stage1(0, 0)
        stage1(0, 1)
        regroup_w(1, 0, "vector")
        regroup_w(1, 1, "scalar")
        quant_x(0, 1, 1)
        transposes(1, 0)
        transposes(1, 1)
        warm_up(2)
        t_out(0, 0)
        t_out(0, 1)
        exit_x(1, 0)
        mix_weights_2()
        quant_w(1, 0)
        quant_w(1, 1)
        exit_x(1, 1)
        small_pe()
        x_terms()
        stage1(0, 2)
        stage1(0, 3)
        quant_x(1, 0, 1)
        transposes(2, 0)
        t_out(0, 2)
        t_out(0, 3)
        transposes(2, 1)

        for k in range(B):
            groups = range(O * H) if k < DIRECT else range(H)
            if k > 0:
                stage2(k - 1, range(H))
            if k + 2 < B:
                exit_x(k + 2, 0)
                exit_x(k + 2, 1)
            for g in groups:
                if k > 0:
                    t_out(k, g)
                if 0 < k < DIRECT and g < H:
                    stage1(k, g + H)
                if k + 1 < B and g >= len(groups) - H:
                    if k + 1 >= DIRECT:
                        planar_pe(k + 1, g - len(groups) + H)
                    stage1(k + 1, g - len(groups) + H)
            if k == 0:
                spread(0)
            if DIRECT <= k + 1 < B and k < 1:
                planar_exits(k + 1)
                regroup_t(k + 1)
            add_x_terms(k, [(0, 0), (0, 1), (1, 0), (1, 1)])
            if k == 0:
                quant_t(0, 0, H)
                quant_x(2, 0, 1)
            elif k < B - 2:
                out_exit(k - 1, range(H))
                quant_t(k, 0, H)
            elif k == B - 2:
                out_exit(k - 1, [0])
                quant_t(k, 0, H)
                out_exit(k - 1, [1])
            else:
                quant_t(k, 0, H)
                out_exit(k - 1, range(H))
            if DIRECT <= k + 1 < B and k >= 1:
                planar_exits(k + 1)
                regroup_t(k + 1)
            if 0 < k < B - 2:
                quant_x(k + 2, 0, 1)
            if k < 0:
                stage2(k, range(H))
            if k + 3 < B:
                transposes(k + 3, 0)
            if k + 3 < B:
                transposes(k + 3, 1)
            if k + 1 < B:
                spread(k + 1)
        stage2(B - 1, range(H))
        out_exit(B - 1, range(H))
